import numpy as np
import ml_dtypes


def mxq(x, axis, fmt="e4m3"):
    dtype, down = {"e4m3": (ml_dtypes.float8_e4m3fn, 7), "e5m2": (ml_dtypes.float8_e5m2, 14)}[fmt]
    v = np.moveaxis(np.asarray(x, np.float32).astype(ml_dtypes.bfloat16).astype(np.float64), axis, -1)
    blocks = v.reshape(v.shape[:-1] + (-1, 32))
    amax = np.abs(blocks).max(-1, keepdims=True)
    byte = np.maximum(np.where(amax > 0, np.frexp(amax)[1] - 1 + 127, 0) - down, 1)
    scale = np.exp2(byte - 127.0)
    codes = (blocks / scale).astype(np.float32).astype(dtype).astype(np.float64)
    return np.moveaxis((codes * scale).reshape(v.shape), -1, axis)


WIDE = False


def mx_kscale(k):
    if not WIDE:
        return np.ones(k)
    levels = np.array([10, -10, 5, -5, 0])
    a = np.random.permutation(np.resize(levels, k // 512 * 4)).reshape(k // 512, 4)
    idx = np.arange(k)
    return np.exp2(a[idx // 512, idx % 128 // 32])


BF16 = ml_dtypes.bfloat16


def bf(x):
    return np.asarray(x, np.float32).astype(BF16)


def f64(x):
    return np.asarray(x).astype(np.float64)


B, D, T = 2, 512, 2048


def setup_inputs():
    s = mx_kscale(D)
    t = s / s.max()
    y = (np.random.standard_normal((B, D, T)) * 2.0 + np.random.standard_normal((B, D, 1)) * 0.7) * t[:, None]
    u = np.random.standard_normal((B, D, T))
    z = np.random.standard_normal((B, D, T))
    return {"x": bf(np.concatenate((y, u, z), axis=1)),
            "W": bf(np.random.standard_normal((D, D)) * 0.3 * np.sqrt(D) / t[:, None])}


def reference(x, W):
    x, W = f64(x), f64(W)
    d = W.shape[0]
    y = np.swapaxes(x[:, :d, :], 1, 2)
    w = np.swapaxes(x[:, d:2 * d, :], 1, 2)
    intensity = np.exp(x[:, d:2 * d, :])
    e = np.exp(w - w.max(-1, keepdims=True))
    sm = e / e.sum(-1, keepdims=True)
    mean = y.mean(axis=1, keepdims=True)
    a = sm * (y - mean)
    rep = (mxq(a, 2, "e4m3") @ mxq(W, 0, "e4m3")) + mean
    rep1 = np.swapaxes(rep, 1, 2)
    y_trans = x[:, 2 * d:3 * d, :] - rep1
    return np.concatenate((rep1, intensity, y_trans), axis=1)

@@ -1,0 +1,309 @@
+from contextlib import ExitStack
+
+import concourse.mybir as mybir
+from concourse.masks import make_identity
+
+FLOPS = 2 * 2 * 2048 * 512 * 512
+
+F32 = mybir.dt.float32
+BF16 = mybir.dt.bfloat16
+U32 = mybir.dt.uint32
+U8 = mybir.dt.uint8
+FP8X4 = mybir.dt.float8_e4m3fn_x4
+ALU = mybir.AluOpType
+ACT = mybir.ActivationFunctionType
+AX = mybir.AxisListType
+
+P = 128
+PACK = 4
+B = 2
+D = 512
+T = 2048
+TC = 512
+NCH = T // TC
+NK = B * NCH
+I_PLAN = [1,1,1,1,1,1,1,0]
+
+
+def tile_crosschannelinterp_kernel(tc, x, W, out):
+    nc = tc.nc
+    with ExitStack() as ctx:
+        ctx.enter_context(nc.allow_non_contiguous_dma(reason="time chunks of channel rows"))
+        const = ctx.enter_context(tc.tile_pool(name="const", bufs=1))
+        work = ctx.enter_context(tc.tile_pool(name="work", bufs=2))
+        small = ctx.enter_context(tc.tile_pool(name="small", bufs=4))
+        outp = ctx.enter_context(tc.tile_pool(name="outp", bufs=2))
+        psum = ctx.enter_context(tc.psum_pool(name="psum", bufs=2))
+        ctx.enter_context(tc.manual_schedule())
+
+        def rows(block, b):
+            return x[b, block * D : (block + 1) * D, :].rearrange("(p j) t -> p j t", j=PACK)
+
+        def out_rows(block, b):
+            return out[b, block * D : (block + 1) * D, :].rearrange("(p j) t -> p j t", j=PACK)
+
+        u = [const.tile([P, PACK, T], BF16, name="u%d" % b) for b in range(B)]
+        y = [const.tile([P, PACK, T], BF16, name="y%d" % b) for b in range(B)]
+        z = [const.tile([P, PACK, T], BF16, name="z%d" % b) for b in range(B)]
+        w_raw = const.tile([P, PACK, D], BF16, name="w_raw")
+
+        def load_u0(c):
+            nc.sync.dma_start(out=u[0][:, :, c * TC : (c + 1) * TC], in_=rows(1, 0)[:, :, c * TC : (c + 1) * TC])
+
+        load_u0(0)
+        nc.sync.dma_start(out=y[0][:, 0:2, :], in_=rows(0, 0)[:, 0:2, :])
+        nc.sync.dma_start(out=y[0][:, 2:4, :], in_=rows(0, 0)[:, 2:4, :])
+        load_u0(1)
+        nc.sync.dma_start(out=w_raw[:], in_=W.rearrange("(p i) j -> p i j", i=PACK))
+        load_u0(2)
+        load_u0(3)
+        nc.sync.dma_start(out=z[0][:], in_=rows(2, 0))
+        nc.sync.dma_start(out=u[1][:], in_=rows(1, 1))
+        nc.sync.dma_start(out=y[1][:], in_=rows(0, 1))
+
+        ident = const.tile([P, P], F32, name="ident")
+        make_identity(nc, ident[:])
+
+        w_grouped = const.tile([P, PACK, P, PACK], BF16, name="w_grouped", align_bytes=64)
+        w_codes = const.tile([P, D], U32, name="w_codes", align_bytes=64)
+        w_scales = const.tile([P, D], U8, name="w_scales", align_bytes=64)
+
+        mean = [const.tile([P, PACK], F32, name="mean%d" % b) for b in range(B)]
+        negmean = [const.tile([P, PACK], F32, name="negmean%d" % b) for b in range(B)]
+        sum_v = [const.tile([P, 2], F32, name="sum_v%d" % b) for b in range(B)]
+        sum_s = [const.tile([P, 2], F32, name="sum_s%d" % b) for b in range(B)]
+
+        def mean_vector(b):
+            nc.vector.tensor_reduce(out=sum_v[b][:], in_=y[b][:, 0:2, :], axis=AX.X, op=ALU.add)
+
+        def mean_scalar(b):
+            for j in range(2, PACK):
+                junk = outp.tile([P, T], F32, name="junk", tag="io", bufs=3)
+                nc.scalar.activation(
+                    out=junk[:], in_=y[b][:, j, :], func=ACT.Identity,
+                    accum_out=sum_s[b][:, j - 2 : j - 1],
+                )
+
+        def mean_finish(b):
+            nc.vector.tensor_scalar(out=mean[b][:, 0:2], in0=sum_v[b][:], scalar1=1.0 / T, scalar2=None, op0=ALU.mult)
+            nc.vector.tensor_scalar(out=mean[b][:, 2:4], in0=sum_s[b][:], scalar1=1.0 / T, scalar2=None, op0=ALU.mult)
+            nc.vector.tensor_scalar(out=negmean[b][:], in0=mean[b][:], scalar1=-1.0, scalar2=None, op0=ALU.mult)
+
+        st = {}
+
+        def where(k):
+            b, c = divmod(k, NCH)
+            return b, c * TC
+
+        def ok(k):
+            return 0 <= k < NK
+
+        def max_j(k):
+            b, t0 = where(k)
+            pair = work.tile([P, 2, TC], BF16, name="pair", tag="pair")
+            nc.vector.tensor_tensor(out=pair[:], in0=u[b][:, 0:2, t0 : t0 + TC], in1=u[b][:, 2:4, t0 : t0 + TC], op=ALU.max)
+            m4 = work.tile([P, TC], BF16, name="m4", tag="m4")
+            nc.vector.tensor_tensor(out=m4[:], in0=pair[:, 0, :], in1=pair[:, 1, :], op=ALU.max)
+            st["m4", k] = m4
+
+        def max_t(k):
+            m_t = psum.tile([P, 2, P], F32, name="m_t", tag="tp")
+            m4w = st["m4", k][:].bitcast(F32)
+            for blk in range(2):
+                nc.tensor.transpose(m_t[:, blk, :], m4w[:, blk * P : (blk + 1) * P], ident[:])
+            st["m_t", k] = m_t
+
+        def max_p(k):
+            top = small.tile([P, 4], F32, name="top", tag="top")
+            nc.vector.tensor_reduce(
+                out=top[:].rearrange("w (b e) -> w b e", e=2),
+                in_=st["m_t", k][:].bitcast(BF16).rearrange("w b (p e) -> w b e p", e=2),
+                axis=AX.X, op=ALU.max,
+            )
+            negm = small.tile([P, 4], F32, name="negm", tag="negm")
+            nc.vector.tensor_scalar(out=negm[:], in0=top[:], scalar1=-1.0, scalar2=None, op0=ALU.mult)
+            st["negm", k] = negm
+
+        def u_t(k, blk):
+            b, t0 = where(k)
+            u32 = u[b][:].bitcast(F32)
+            t_u = psum.tile([P, PACK, P], F32, name="t_u", tag="tp")
+            w0 = t0 // 2 + blk * P
+            for j in range(PACK):
+                nc.tensor.transpose(t_u[:, j, :], u32[:, j, w0 : w0 + P], ident[:])
+            st["t_u", k, blk] = t_u
+
+        def front(k):
+            max_j(k)
+            max_t(k)
+            u_t(k, 0)
+            max_p(k)
+            u_t(k, 1)
+
+        def exps(k):
+            negm = st["negm", k]
+            e_t = work.tile([P, 4, PACK, P], F32, name="e_t", tag="e_t", bufs=3)
+            ssum = small.tile([P, 4], F32, name="ssum", tag="ssum")
+            for blk in range(2):
+                v = st["t_u", k, blk][:].bitcast(BF16).rearrange("w j (p e) -> w e j p", e=2)
+                for e in range(2):
+                    i = blk * 2 + e
+                    nc.scalar.activation(
+                        out=e_t[:, i, :, :], in_=v[:, e, :, :], func=ACT.Exp,
+                        bias=negm[:, i : i + 1], scale=1.0, accum_out=ssum[:, i : i + 1],
+                    )
+            st["e_t", k] = e_t
+            st["ssum", k] = ssum
+
+        def centre(k, on_vector):
+            b, t0 = where(k)
+            ym = work.tile([P, PACK, TC], F32, name="ym", tag="ym")
+            for j in range(PACK):
+                if on_vector:
+                    nc.vector.tensor_scalar(
+                        out=ym[:, j, :], in0=y[b][:, j, t0 : t0 + TC],
+                        scalar1=negmean[b][:, j : j + 1], scalar2=None, op0=ALU.add,
+                    )
+                else:
+                    nc.gpsimd.tensor_scalar(
+                        out=ym[:, j, :], in0=y[b][:, j, t0 : t0 + TC],
+                        scalar1=negmean[b][:, j : j + 1], scalar2=1.0, op0=ALU.add, op1=ALU.mult,
+                    )
+            st["ym", k] = ym
+
+        def normalise(k):
+            rinv = small.tile([P, 4], F32, name="rinv", tag="rinv")
+            nc.vector.reciprocal(out=rinv[:], in_=st["ssum", k][:])
+            e_t = st["e_t", k]
+            for i in range(4):
+                nc.gpsimd.tensor_scalar(
+                    out=e_t[:, i, :, :], in0=e_t[:, i, :, :],
+                    scalar1=rinv[:, i : i + 1], scalar2=0.0, op0=ALU.mult, op1=ALU.add,
+                )
+
+        def back(k, i):
+            e_t = st["e_t", k]
+            s_b = psum.tile([P, PACK, P], F32, name="s_b", tag="s_b")
+            for j in range(PACK):
+                nc.tensor.transpose(s_b[:, j, :], e_t[:, i, j, :], ident[:])
+            st["s_b", k, i] = s_b
+
+        def product(k, i):
+            if i == 0:
+                st["a_g", k] = work.tile([P, TC, PACK], BF16, name="a_g", tag="a_g", align_bytes=64)
+            a_g = st["a_g", k]
+            ymv = st["ym", k][:].rearrange("p j (b w e) -> p b e w j", b=2, e=2)
+            blk, e = divmod(i, 2)
+            n0 = e * 256 + blk * P
+            nc.vector.tensor_tensor(
+                out=a_g[:, n0 : n0 + P, :], in0=ymv[:, blk, e, :, :],
+                in1=st["s_b", k, i][:].rearrange("p j w -> p w j"), op=ALU.mult,
+            )
+
+        def quantise_and_multiply(k):
+            codes = work.tile([P, TC], U32, name="codes", tag="codes", align_bytes=64)
+            scales = work.tile([P, TC], U8, name="scales", tag="scales", align_bytes=64)
+            nc.vector.quantize_mx(
+                out=codes[:].bitcast(FP8X4), scales=scales[:],
+                in_=st["a_g", k][:].rearrange("p n j -> p (n j)"),
+            )
+            for jb in range(PACK):
+                acc = psum.tile([P, TC], F32, name="acc", tag="acc", bufs=4)
+                nc.tensor.matmul_mx(
+                    out=acc[:],
+                    lhsT=w_codes[:, jb * P : (jb + 1) * P].bitcast(FP8X4),
+                    lhsT_scale=w_scales[:, jb * P : (jb + 1) * P],
+                    rhs=codes[:].bitcast(FP8X4), rhs_scale=scales[:],
+                    start=True, stop=True,
+                )
+                st["acc", k, jb] = acc
+
+        def residual(k):
+            b, t0 = where(k)
+            ytr = outp.tile([P, PACK, TC], F32, name="ytr", tag="ytr")
+            for jb in range(PACK):
+                nc.vector.scalar_tensor_tensor(
+                    out=ytr[:, jb, :].rearrange("m (w e) -> m w e", e=2),
+                    in0=z[b][:, jb, t0 : t0 + TC].rearrange("m (w e) -> m w e", e=2),
+                    scalar=mean[b][:, jb : jb + 1],
+                    in1=st["acc", k, jb][:].rearrange("m (e w) -> m w e", e=2),
+                    op0=ALU.subtract, op1=ALU.subtract,
+                )
+            nc.sync.dma_start(out=out_rows(2, b)[:, :, t0 : t0 + TC], in_=ytr[:])
+
+        def representation(k):
+            b, t0 = where(k)
+            rep = outp.tile([P, PACK, TC], F32, name="rep", tag="rep")
+            for jb in range(PACK):
+                nc.scalar.activation(
+                    out=rep[:, jb, :].rearrange("m (w e) -> m w e", e=2),
+                    in_=st["acc", k, jb][:].rearrange("m (e w) -> m w e", e=2),
+                    func=ACT.Identity, bias=mean[b][:, jb : jb + 1], scale=1.0,
+                )
+            nc.sync.dma_start(out=out_rows(0, b)[:, :, t0 : t0 + TC], in_=rep[:])
+
+        todo = list(range(B * PACK))
+
+        def intensity(count):
+            for r in todo[:count]:
+                b, j = divmod(r, PACK)
+                io = outp.tile([P, T], F32, name="io", tag="io", bufs=3)
+                nc.scalar.activation(out=io[:], in_=u[b][:, j, :], func=ACT.Exp)
+                nc.sync.dma_start(out=out_rows(1, b)[:, j, :], in_=io[:])
+            todo[:count] = []
+
+        front(0)
+        exps(0)
+        mean_vector(0)
+        mean_scalar(0)
+        normalise(0)
+        front(1)
+        mean_finish(0)
+        centre(0, True)
+        nc.scalar.copy(out=w_grouped[:], in_=w_raw[:].rearrange("p i (m jb) -> p jb m i", jb=PACK))
+        exps(1)
+        back(0, 0)
+        back(0, 1)
+        centre(1, False)
+        for k in range(NK):
+            product(k, 0)
+            back(k, 2)
+            product(k, 1)
+            back(k, 3)
+            if k == 0:
+                nc.vector.quantize_mx(
+                    out=w_codes[:].bitcast(FP8X4), scales=w_scales[:],
+                    in_=w_grouped[:].rearrange("p jb m i -> p (jb m i)"),
+                )
+            if ok(k + 2):
+                max_j(k + 2)
+                max_t(k + 2)
+                u_t(k + 2, 0)
+            product(k, 2)
+            product(k, 3)
+            quantise_and_multiply(k)
+            if ok(k + 1):
+                normalise(k + 1)
+            if ok(k + 2):
+                max_p(k + 2)
+                u_t(k + 2, 1)
+            if ok(k + 1):
+                back(k + 1, 0)
+                back(k + 1, 1)
+            if k == 0:
+                intensity(1)
+            if ok(k + 2):
+                exps(k + 2)
+            if k == 1:
+                mean_scalar(1)
+            if ok(k + 2):
+                centre(k + 2, False)
+            residual(k)
+            if k == 1:
+                mean_vector(1)
+                mean_finish(1)
+            representation(k)
+            if k == 0:
+                nc.sync.dma_start(out=z[1][:], in_=rows(2, 1))
+            intensity(I_PLAN[k])
+        intensity(len(todo))

@@ -22,7 +22,6 @@ T = 2048
 TC = 512
 NCH = T // TC
 NK = B * NCH
-I_PLAN = [1,1,1,1,1,1,1,0]
 
 
 def tile_crosschannelinterp_kernel(tc, x, W, out):
@@ -54,35 +53,46 @@ def tile_crosschannelinterp_kernel(tc, x, W, out):
         nc.sync.dma_start(out=y[0][:, 0:2, :], in_=rows(0, 0)[:, 0:2, :])
         nc.sync.dma_start(out=y[0][:, 2:4, :], in_=rows(0, 0)[:, 2:4, :])
         load_u0(1)
-        nc.sync.dma_start(out=w_raw[:], in_=W.rearrange("(p i) j -> p i j", i=PACK))
         load_u0(2)
+        nc.sync.dma_start(out=w_raw[:], in_=W.rearrange("(p i) j -> p i j", i=PACK))
         load_u0(3)
-        nc.sync.dma_start(out=z[0][:], in_=rows(2, 0))
         nc.sync.dma_start(out=u[1][:], in_=rows(1, 1))
+        nc.sync.dma_start(out=z[0][:], in_=rows(2, 0))
         nc.sync.dma_start(out=y[1][:], in_=rows(0, 1))
+        nc.sync.dma_start(out=z[1][:], in_=rows(2, 1))
 
         ident = const.tile([P, P], F32, name="ident")
         make_identity(nc, ident[:])
+        warm = const.tile([P, 1], F32, name="warm")
+        nc.scalar.activation(out=warm[:], in_=ident[:, 0:1], func=ACT.Exp)
 
         w_grouped = const.tile([P, PACK, P, PACK], BF16, name="w_grouped", align_bytes=64)
         w_codes = const.tile([P, D], U32, name="w_codes", align_bytes=64)
         w_scales = const.tile([P, D], U8, name="w_scales", align_bytes=64)
+
+        def group_w():
+            nc.scalar.copy(out=w_grouped[:], in_=w_raw[:].rearrange("p i (m jb) -> p jb m i", jb=PACK))
+
+        def quantise_w():
+            nc.vector.quantize_mx(
+                out=w_codes[:].bitcast(FP8X4), scales=w_scales[:],
+                in_=w_grouped[:].rearrange("p jb m i -> p (jb m i)"),
+            )
 
         mean = [const.tile([P, PACK], F32, name="mean%d" % b) for b in range(B)]
         negmean = [const.tile([P, PACK], F32, name="negmean%d" % b) for b in range(B)]
         sum_v = [const.tile([P, 2], F32, name="sum_v%d" % b) for b in range(B)]
         sum_s = [const.tile([P, 2], F32, name="sum_s%d" % b) for b in range(B)]
 
-        def mean_vector(b):
-            nc.vector.tensor_reduce(out=sum_v[b][:], in_=y[b][:, 0:2, :], axis=AX.X, op=ALU.add)
+        def mean_vector(b, j):
+            nc.vector.tensor_reduce(out=sum_v[b][:, j : j + 1], in_=y[b][:, j, :], axis=AX.X, op=ALU.add)
 
-        def mean_scalar(b):
-            for j in range(2, PACK):
-                junk = outp.tile([P, T], F32, name="junk", tag="io", bufs=3)
-                nc.scalar.activation(
-                    out=junk[:], in_=y[b][:, j, :], func=ACT.Identity,
-                    accum_out=sum_s[b][:, j - 2 : j - 1],
-                )
+        def mean_scalar(b, j):
+            junk = outp.tile([P, T], F32, name="junk", tag="io", bufs=3)
+            nc.scalar.activation(
+                out=junk[:], in_=y[b][:, j, :], func=ACT.Identity,
+                accum_out=sum_s[b][:, j - 2 : j - 1],
+            )
 
         def mean_finish(b):
             nc.vector.tensor_scalar(out=mean[b][:, 0:2], in0=sum_v[b][:], scalar1=1.0 / T, scalar2=None, op0=ALU.mult)
@@ -104,11 +114,8 @@ def tile_crosschannelinterp_kernel(tc, x, W, out):
             nc.vector.tensor_tensor(out=pair[:], in0=u[b][:, 0:2, t0 : t0 + TC], in1=u[b][:, 2:4, t0 : t0 + TC], op=ALU.max)
             m4 = work.tile([P, TC], BF16, name="m4", tag="m4")
             nc.vector.tensor_tensor(out=m4[:], in0=pair[:, 0, :], in1=pair[:, 1, :], op=ALU.max)
-            st["m4", k] = m4
-
-        def max_t(k):
             m_t = psum.tile([P, 2, P], F32, name="m_t", tag="tp")
-            m4w = st["m4", k][:].bitcast(F32)
+            m4w = m4[:].bitcast(F32)
             for blk in range(2):
                 nc.tensor.transpose(m_t[:, blk, :], m4w[:, blk * P : (blk + 1) * P], ident[:])
             st["m_t", k] = m_t
@@ -132,13 +139,6 @@ def tile_crosschannelinterp_kernel(tc, x, W, out):
             for j in range(PACK):
                 nc.tensor.transpose(t_u[:, j, :], u32[:, j, w0 : w0 + P], ident[:])
             st["t_u", k, blk] = t_u
-
-        def front(k):
-            max_j(k)
-            max_t(k)
-            u_t(k, 0)
-            max_p(k)
-            u_t(k, 1)
 
         def exps(k):
             negm = st["negm", k]
@@ -200,110 +200,166 @@ def tile_crosschannelinterp_kernel(tc, x, W, out):
                 in1=st["s_b", k, i][:].rearrange("p j w -> p w j"), op=ALU.mult,
             )
 
-        def quantise_and_multiply(k):
+        def quantise(k):
             codes = work.tile([P, TC], U32, name="codes", tag="codes", align_bytes=64)
             scales = work.tile([P, TC], U8, name="scales", tag="scales", align_bytes=64)
             nc.vector.quantize_mx(
                 out=codes[:].bitcast(FP8X4), scales=scales[:],
                 in_=st["a_g", k][:].rearrange("p n j -> p (n j)"),
             )
-            for jb in range(PACK):
-                acc = psum.tile([P, TC], F32, name="acc", tag="acc", bufs=4)
-                nc.tensor.matmul_mx(
-                    out=acc[:],
-                    lhsT=w_codes[:, jb * P : (jb + 1) * P].bitcast(FP8X4),
-                    lhsT_scale=w_scales[:, jb * P : (jb + 1) * P],
-                    rhs=codes[:].bitcast(FP8X4), rhs_scale=scales[:],
-                    start=True, stop=True,
-                )
-                st["acc", k, jb] = acc
+            st["codes", k] = codes
+            st["scales", k] = scales
 
-        def residual(k):
-            b, t0 = where(k)
-            ytr = outp.tile([P, PACK, TC], F32, name="ytr", tag="ytr")
-            for jb in range(PACK):
-                nc.vector.scalar_tensor_tensor(
-                    out=ytr[:, jb, :].rearrange("m (w e) -> m w e", e=2),
-                    in0=z[b][:, jb, t0 : t0 + TC].rearrange("m (w e) -> m w e", e=2),
-                    scalar=mean[b][:, jb : jb + 1],
-                    in1=st["acc", k, jb][:].rearrange("m (e w) -> m w e", e=2),
-                    op0=ALU.subtract, op1=ALU.subtract,
-                )
-            nc.sync.dma_start(out=out_rows(2, b)[:, :, t0 : t0 + TC], in_=ytr[:])
+        def multiply(k, jb):
+            acc = psum.tile([P, TC], F32, name="acc", tag="acc", bufs=4)
+            nc.tensor.matmul_mx(
+                out=acc[:],
+                lhsT=w_codes[:, jb * P : (jb + 1) * P].bitcast(FP8X4),
+                lhsT_scale=w_scales[:, jb * P : (jb + 1) * P],
+                rhs=st["codes", k][:].bitcast(FP8X4), rhs_scale=st["scales", k][:],
+                start=True, stop=True,
+            )
+            st["acc", k, jb] = acc
 
-        def representation(k):
+        def residual(k, jb):
             b, t0 = where(k)
-            rep = outp.tile([P, PACK, TC], F32, name="rep", tag="rep")
-            for jb in range(PACK):
-                nc.scalar.activation(
-                    out=rep[:, jb, :].rearrange("m (w e) -> m w e", e=2),
-                    in_=st["acc", k, jb][:].rearrange("m (e w) -> m w e", e=2),
-                    func=ACT.Identity, bias=mean[b][:, jb : jb + 1], scale=1.0,
-                )
-            nc.sync.dma_start(out=out_rows(0, b)[:, :, t0 : t0 + TC], in_=rep[:])
+            if st.get(("ytr", k)) is None:
+                st["ytr", k] = outp.tile([P, PACK, TC], F32, name="ytr", tag="ytr")
+            nc.vector.scalar_tensor_tensor(
+                out=st["ytr", k][:, jb, :].rearrange("m (w e) -> m w e", e=2),
+                in0=z[b][:, jb, t0 : t0 + TC].rearrange("m (w e) -> m w e", e=2),
+                scalar=mean[b][:, jb : jb + 1],
+                in1=st["acc", k, jb][:].rearrange("m (e w) -> m w e", e=2),
+                op0=ALU.subtract, op1=ALU.subtract,
+            )
+
+        def store_residual(k):
+            b, t0 = where(k)
+            nc.sync.dma_start(out=out_rows(2, b)[:, :, t0 : t0 + TC], in_=st["ytr", k][:])
+
+        def representation(k, jb):
+            b, t0 = where(k)
+            if st.get(("rep", k)) is None:
+                st["rep", k] = outp.tile([P, PACK, TC], F32, name="rep", tag="rep")
+            nc.scalar.activation(
+                out=st["rep", k][:, jb, :].rearrange("m (w e) -> m w e", e=2),
+                in_=st["acc", k, jb][:].rearrange("m (e w) -> m w e", e=2),
+                func=ACT.Identity, bias=mean[b][:, jb : jb + 1], scale=1.0,
+            )
+
+        def store_representation(k):
+            b, t0 = where(k)
+            nc.sync.dma_start(out=out_rows(0, b)[:, :, t0 : t0 + TC], in_=st["rep", k][:])
 
         todo = list(range(B * PACK))
 
-        def intensity(count):
-            for r in todo[:count]:
-                b, j = divmod(r, PACK)
-                io = outp.tile([P, T], F32, name="io", tag="io", bufs=3)
-                nc.scalar.activation(out=io[:], in_=u[b][:, j, :], func=ACT.Exp)
-                nc.sync.dma_start(out=out_rows(1, b)[:, j, :], in_=io[:])
-            todo[:count] = []
+        def intensity():
+            b, j = divmod(todo[0], PACK)
+            todo[:1] = []
+            io = outp.tile([P, T], F32, name="io", tag="io", bufs=3)
+            nc.scalar.activation(out=io[:], in_=u[b][:, j, :], func=ACT.Exp)
+            nc.sync.dma_start(out=out_rows(1, b)[:, j, :], in_=io[:])
 
-        front(0)
-        exps(0)
-        mean_vector(0)
-        mean_scalar(0)
-        normalise(0)
-        front(1)
-        mean_finish(0)
-        centre(0, True)
-        nc.scalar.copy(out=w_grouped[:], in_=w_raw[:].rearrange("p i (m jb) -> p jb m i", jb=PACK))
-        exps(1)
-        back(0, 0)
-        back(0, 1)
-        centre(1, False)
-        for k in range(NK):
-            product(k, 0)
-            back(k, 2)
-            product(k, 1)
-            back(k, 3)
-            if k == 0:
-                nc.vector.quantize_mx(
-                    out=w_codes[:].bitcast(FP8X4), scales=w_scales[:],
-                    in_=w_grouped[:].rearrange("p jb m i -> p (jb m i)"),
-                )
-            if ok(k + 2):
-                max_j(k + 2)
-                max_t(k + 2)
-                u_t(k + 2, 0)
-            product(k, 2)
-            product(k, 3)
-            quantise_and_multiply(k)
-            if ok(k + 1):
-                normalise(k + 1)
-            if ok(k + 2):
-                max_p(k + 2)
-                u_t(k + 2, 1)
-            if ok(k + 1):
-                back(k + 1, 0)
-                back(k + 1, 1)
-            if k == 0:
-                intensity(1)
+        for k in range(-3, NK + 1):
+            if k == 6:
+                intensity()
+            if ok(k):
+                product(k, 0)
+            if k == -1:
+                mean_vector(0, 0)
+            if k == -1:
+                mean_scalar(0, 2)
+            if k == 7:
+                intensity()
             if ok(k + 2):
                 exps(k + 2)
-            if k == 1:
-                mean_scalar(1)
-            if ok(k + 2):
-                centre(k + 2, False)
-            residual(k)
-            if k == 1:
-                mean_vector(1)
-                mean_finish(1)
-            representation(k)
+            if ok(k):
+                back(k, 2)
+            if k == 2:
+                mean_scalar(1, 2)
+            if ok(k + 3):
+                max_j(k + 3)
+            if k == 3:
+                intensity()
+            if ok(k):
+                product(k, 1)
             if k == 0:
-                nc.sync.dma_start(out=z[1][:], in_=rows(2, 1))
-            intensity(I_PLAN[k])
-        intensity(len(todo))
+                quantise_w()
+            if ok(k - 1):
+                residual(k - 1, 0)
+            if k == -2:
+                mean_scalar(0, 3)
+            if k == 1:
+                mean_vector(1, 1)
+            if ok(k):
+                product(k, 2)
+            if k == -1:
+                mean_finish(0)
+            if ok(k - 1):
+                representation(k - 1, 2)
+            if k == 0:
+                intensity()
+            if ok(k + 3):
+                max_p(k + 3)
+            if k == 2:
+                mean_finish(1)
+            if ok(k):
+                back(k, 3)
+            if ok(k):
+                product(k, 3)
+            if ok(k - 1):
+                representation(k - 1, 1)
+            if ok(k + 2):
+                normalise(k + 2)
+            if k == 0:
+                intensity()
+            if ok(k):
+                quantise(k)
+            if k == -1:
+                group_w()
+            if ok(k + 3):
+                u_t(k + 3, 0)
+            if ok(k - 1):
+                representation(k - 1, 3)
+            if k == 0:
+                intensity()
+            if ok(k - 1):
+                residual(k - 1, 2)
+            if ok(k - 1):
+                representation(k - 1, 0)
+            if k == -1:
+                centre(0, True)
+            if ok(k + 1):
+                back(k + 1, 0)
+            if ok(k - 1):
+                store_representation(k - 1)
+            if k == 1:
+                mean_scalar(1, 3)
+            if ok(k + 3):
+                u_t(k + 3, 1)
+            if ok(k + 1):
+                back(k + 1, 1)
+            if ok(k + 2) and k + 2 > 0:
+                centre(k + 2, False)
+            if ok(k):
+                multiply(k, 0)
+            if ok(k - 1):
+                residual(k - 1, 1)
+            if ok(k):
+                multiply(k, 2)
+            if k == -3:
+                mean_vector(0, 1)
+            if ok(k - 1):
+                residual(k - 1, 3)
+            if k == 4:
+                intensity()
+            if ok(k):
+                multiply(k, 1)
+            if k == 3:
+                intensity()
+            if ok(k - 1):
+                store_residual(k - 1)
+            if k == 0:
+                mean_vector(1, 0)
+            if ok(k):
+                multiply(k, 3)

@@ -81,23 +81,30 @@ def tile_crosschannelinterp_kernel(tc, x, W, out):
 
         mean = [const.tile([P, PACK], F32, name="mean%d" % b) for b in range(B)]
         negmean = [const.tile([P, PACK], F32, name="negmean%d" % b) for b in range(B)]
-        sum_v = [const.tile([P, 2], F32, name="sum_v%d" % b) for b in range(B)]
-        sum_s = [const.tile([P, 2], F32, name="sum_s%d" % b) for b in range(B)]
+        sum_v = const.tile([P, B, PACK], F32, name="sum_v")
+        sum_s = const.tile([P, B, PACK], F32, name="sum_s")
+        nc.vector.memset(sum_v[:], 0.0)
+        nc.vector.memset(sum_s[:], 0.0)
 
         def mean_vector(b, j):
-            nc.vector.tensor_reduce(out=sum_v[b][:, j : j + 1], in_=y[b][:, j, :], axis=AX.X, op=ALU.add)
+            nc.vector.tensor_reduce(out=sum_v[:, b, j : j + 1], in_=y[b][:, j, :], axis=AX.X, op=ALU.add)
 
         def mean_scalar(b, j):
             junk = outp.tile([P, T], F32, name="junk", tag="io", bufs=3)
             nc.scalar.activation(
-                out=junk[:], in_=y[b][:, j, :], func=ACT.Identity,
-                accum_out=sum_s[b][:, j - 2 : j - 1],
+                out=junk[:], in_=y[b][:, j, :], func=ACT.Identity, scale=1.0 / T,
+                accum_out=sum_s[:, b, j : j + 1],
             )
 
         def mean_finish(b):
-            nc.vector.tensor_scalar(out=mean[b][:, 0:2], in0=sum_v[b][:], scalar1=1.0 / T, scalar2=None, op0=ALU.mult)
-            nc.vector.tensor_scalar(out=mean[b][:, 2:4], in0=sum_s[b][:], scalar1=1.0 / T, scalar2=None, op0=ALU.mult)
-            nc.vector.tensor_scalar(out=negmean[b][:], in0=mean[b][:], scalar1=-1.0, scalar2=None, op0=ALU.mult)
+            nc.vector.scalar_tensor_tensor(
+                out=negmean[b][:], in0=sum_v[:, b, :], scalar=-1.0 / T, in1=sum_s[:, b, :],
+                op0=ALU.mult, op1=ALU.subtract,
+            )
+            nc.vector.scalar_tensor_tensor(
+                out=mean[b][:], in0=sum_v[:, b, :], scalar=1.0 / T, in1=sum_s[:, b, :],
+                op0=ALU.mult, op1=ALU.add,
+            )
 
         st = {}
 
@@ -121,14 +128,12 @@ def tile_crosschannelinterp_kernel(tc, x, W, out):
             st["m_t", k] = m_t
 
         def max_p(k):
-            top = small.tile([P, 4], F32, name="top", tag="top")
-            nc.vector.tensor_reduce(
-                out=top[:].rearrange("w (b e) -> w b e", e=2),
-                in_=st["m_t", k][:].bitcast(BF16).rearrange("w b (p e) -> w b e p", e=2),
-                axis=AX.X, op=ALU.max,
-            )
             negm = small.tile([P, 4], F32, name="negm", tag="negm")
-            nc.vector.tensor_scalar(out=negm[:], in0=top[:], scalar1=-1.0, scalar2=None, op0=ALU.mult)
+            nc.vector.tensor_reduce(
+                out=negm[:].rearrange("w (b e) -> w b e", e=2),
+                in_=st["m_t", k][:].bitcast(BF16).rearrange("w b (p e) -> w b e p", e=2),
+                axis=AX.X, op=ALU.max, negate=True,
+            )
             st["negm", k] = negm
 
         def u_t(k, blk):
@@ -261,105 +266,105 @@ def tile_crosschannelinterp_kernel(tc, x, W, out):
             nc.sync.dma_start(out=out_rows(1, b)[:, j, :], in_=io[:])
 
         for k in range(-3, NK + 1):
+            if k == -1:
+                mean_finish(0)
+            if ok(k):
+                product(k, 0)
             if k == 6:
                 intensity()
             if ok(k):
-                product(k, 0)
-            if k == -1:
-                mean_vector(0, 0)
-            if k == -1:
-                mean_scalar(0, 2)
-            if k == 7:
-                intensity()
+                back(k, 2)
             if ok(k + 2):
                 exps(k + 2)
-            if ok(k):
-                back(k, 2)
-            if k == 2:
-                mean_scalar(1, 2)
             if ok(k + 3):
                 max_j(k + 3)
-            if k == 3:
-                intensity()
-            if ok(k):
-                product(k, 1)
-            if k == 0:
-                quantise_w()
-            if ok(k - 1):
-                residual(k - 1, 0)
-            if k == -2:
-                mean_scalar(0, 3)
-            if k == 1:
-                mean_vector(1, 1)
-            if ok(k):
-                product(k, 2)
-            if k == -1:
-                mean_finish(0)
-            if ok(k - 1):
-                representation(k - 1, 2)
             if k == 0:
                 intensity()
-            if ok(k + 3):
-                max_p(k + 3)
-            if k == 2:
-                mean_finish(1)
-            if ok(k):
-                back(k, 3)
-            if ok(k):
-                product(k, 3)
-            if ok(k - 1):
-                representation(k - 1, 1)
-            if ok(k + 2):
-                normalise(k + 2)
-            if k == 0:
-                intensity()
-            if ok(k):
-                quantise(k)
-            if k == -1:
-                group_w()
-            if ok(k + 3):
-                u_t(k + 3, 0)
-            if ok(k - 1):
-                representation(k - 1, 3)
-            if k == 0:
-                intensity()
-            if ok(k - 1):
-                residual(k - 1, 2)
             if ok(k - 1):
                 representation(k - 1, 0)
-            if k == -1:
-                centre(0, True)
-            if ok(k + 1):
-                back(k + 1, 0)
-            if ok(k - 1):
-                store_representation(k - 1)
             if k == 1:
-                mean_scalar(1, 3)
-            if ok(k + 3):
-                u_t(k + 3, 1)
-            if ok(k + 1):
-                back(k + 1, 1)
-            if ok(k + 2) and k + 2 > 0:
-                centre(k + 2, False)
-            if ok(k):
-                multiply(k, 0)
-            if ok(k - 1):
-                residual(k - 1, 1)
-            if ok(k):
-                multiply(k, 2)
-            if k == -3:
-                mean_vector(0, 1)
-            if ok(k - 1):
-                residual(k - 1, 3)
+                mean_scalar(1, 0)
             if k == 4:
                 intensity()
             if ok(k):
-                multiply(k, 1)
+                product(k, 1)
+            if k == -2:
+                mean_scalar(0, 2)
+            if ok(k - 1):
+                residual(k - 1, 0)
             if k == 3:
                 intensity()
+            if ok(k):
+                back(k, 3)
+            if k == -1:
+                centre(0, True)
+            if k == 3:
+                intensity()
+            if ok(k):
+                product(k, 2)
+            if k == -2:
+                mean_vector(0, 3)
             if ok(k - 1):
-                store_residual(k - 1)
+                representation(k - 1, 2)
             if k == 0:
-                mean_vector(1, 0)
+                quantise_w()
+            if ok(k + 3):
+                max_p(k + 3)
+            if ok(k + 1):
+                back(k + 1, 0)
+            if ok(k + 3):
+                u_t(k + 3, 0)
+            if ok(k):
+                product(k, 3)
+            if ok(k + 2):
+                normalise(k + 2)
+            if k == 2:
+                mean_scalar(1, 2)
+            if k == 2:
+                mean_finish(1)
+            if ok(k - 1):
+                representation(k - 1, 1)
+            if k == -1:
+                group_w()
+            if ok(k - 1):
+                representation(k - 1, 3)
+            if k == 1:
+                mean_scalar(1, 3)
+            if ok(k):
+                quantise(k)
+            if k == -2:
+                intensity()
+            if ok(k - 1):
+                residual(k - 1, 2)
+            if k == -3:
+                mean_vector(0, 0)
+            if ok(k + 3):
+                u_t(k + 3, 1)
+            if ok(k - 1):
+                residual(k - 1, 1)
+            if ok(k - 1):
+                store_representation(k - 1)
+            if k == 5:
+                intensity()
+            if ok(k):
+                multiply(k, 0)
+            if k == 6:
+                intensity()
+            if ok(k - 1):
+                residual(k - 1, 3)
+            if ok(k + 2) and k + 2 > 0:
+                centre(k + 2, False)
+            if ok(k + 1):
+                back(k + 1, 1)
+            if ok(k):
+                multiply(k, 2)
+            if ok(k):
+                multiply(k, 1)
             if ok(k):
                 multiply(k, 3)
+            if ok(k - 1):
+                store_residual(k - 1)
+            if k == -3:
+                mean_scalar(0, 1)
+            if k == 0:
+                mean_vector(1, 1)

@@ -71,7 +71,10 @@ def tile_crosschannelinterp_kernel(tc, x, W, out):
         w_scales = const.tile([P, D], U8, name="w_scales", align_bytes=64)
 
         def group_w():
-            nc.scalar.copy(out=w_grouped[:], in_=w_raw[:].rearrange("p i (m jb) -> p jb m i", jb=PACK))
+            nc.gpsimd.tensor_scalar(
+                out=w_grouped[:], in0=w_raw[:].rearrange("p i (m jb) -> p jb m i", jb=PACK),
+                scalar1=1.0, scalar2=0.0, op0=ALU.mult, op1=ALU.add,
+            )
 
         def quantise_w():
             nc.vector.quantize_mx(
@@ -318,14 +321,14 @@ def tile_crosschannelinterp_kernel(tc, x, W, out):
                 product(k, 3)
             if ok(k + 2):
                 normalise(k + 2)
+            if k == -2:
+                group_w()
             if k == 2:
                 mean_scalar(1, 2)
             if k == 2:
                 mean_finish(1)
             if ok(k - 1):
                 representation(k - 1, 1)
-            if k == -1:
-                group_w()
             if ok(k - 1):
                 representation(k - 1, 3)
             if k == 1:

@@ -22,6 +22,13 @@ T = 2048
 TC = 512
 NCH = T // TC
 NK = B * NCH
+FILL = {0: 1, 3: 1, 4: 1, 5: 1, 6: 1}
+HEAD_FILL = 3
+Z1_AFTER = 1
+MEAN1 = {1: (0,), 2: (1,)}
+MEAN1V = {1: (2,), 2: (3,)}
+LOADS0 = ("u0a", "u0b", "y0a", "y0b", "W", "z0")
+LOADS1 = ("u1", "y1", "z1")
 
 
 def tile_crosschannelinterp_kernel(tc, x, W, out):
@@ -46,20 +53,38 @@ def tile_crosschannelinterp_kernel(tc, x, W, out):
         z = [const.tile([P, PACK, T], BF16, name="z%d" % b) for b in range(B)]
         w_raw = const.tile([P, PACK, D], BF16, name="w_raw")
 
-        def load_u0(c):
-            nc.sync.dma_start(out=u[0][:, :, c * TC : (c + 1) * TC], in_=rows(1, 0)[:, :, c * TC : (c + 1) * TC])
+        def load(name):
+            if name == "u0a":
+                nc.sync.dma_start(out=u[0][:, :, 0:TC], in_=rows(1, 0)[:, :, 0:TC])
+            if name == "u0b":
+                nc.sync.dma_start(out=u[0][:, :, TC:T], in_=rows(1, 0)[:, :, TC:T])
+            if name == "u0c1":
+                nc.sync.dma_start(out=u[0][:, :, TC:2*TC], in_=rows(1, 0)[:, :, TC:2*TC])
+            if name == "u0c23":
+                nc.sync.dma_start(out=u[0][:, :, 2*TC:T], in_=rows(1, 0)[:, :, 2*TC:T])
+            if name == "y0a":
+                nc.sync.dma_start(out=y[0][:, 0:2, :], in_=rows(0, 0)[:, 0:2, :])
+            if name == "y0b":
+                nc.sync.dma_start(out=y[0][:, 2:4, :], in_=rows(0, 0)[:, 2:4, :])
+            if name == "W":
+                nc.sync.dma_start(out=w_raw[:], in_=W.rearrange("(p i) j -> p i j", i=PACK))
+            if name == "z0":
+                nc.sync.dma_start(out=z[0][:], in_=rows(2, 0))
+            if name == "u1":
+                nc.sync.dma_start(out=u[1][:], in_=rows(1, 1))
+            if name == "y1":
+                nc.sync.dma_start(out=y[1][:], in_=rows(0, 1))
+            if name == "z1":
+                nc.sync.dma_start(out=z[1][:], in_=rows(2, 1))
 
-        load_u0(0)
-        nc.sync.dma_start(out=y[0][:, 0:2, :], in_=rows(0, 0)[:, 0:2, :])
-        nc.sync.dma_start(out=y[0][:, 2:4, :], in_=rows(0, 0)[:, 2:4, :])
-        load_u0(1)
-        load_u0(2)
-        nc.sync.dma_start(out=w_raw[:], in_=W.rearrange("(p i) j -> p i j", i=PACK))
-        load_u0(3)
-        nc.sync.dma_start(out=u[1][:], in_=rows(1, 1))
-        nc.sync.dma_start(out=z[0][:], in_=rows(2, 0))
-        nc.sync.dma_start(out=y[1][:], in_=rows(0, 1))
-        nc.sync.dma_start(out=z[1][:], in_=rows(2, 1))
+        for name in LOADS0:
+            load(name)
+        later = list(LOADS1)
+
+        def next_load():
+            if later:
+                load(later[0])
+                later[:1] = []
 
         ident = const.tile([P, P], F32, name="ident")
         make_identity(nc, ident[:])
@@ -90,10 +115,14 @@ def tile_crosschannelinterp_kernel(tc, x, W, out):
         nc.vector.memset(sum_s[:], 0.0)
 
         def mean_vector(b, j):
-            nc.vector.tensor_reduce(out=sum_v[:, b, j : j + 1], in_=y[b][:, j, :], axis=AX.X, op=ALU.add)
+            junk2 = work.tile([P, T], BF16, name="junk2", tag="junk2", bufs=1)
+            nc.vector.tensor_scalar(
+                out=junk2[:], in0=y[b][:, j, :], scalar1=1.0, scalar2=None, op0=ALU.mult, op1=ALU.add,
+                accum_out=sum_v[:, b, j : j + 1],
+            )
 
         def mean_scalar(b, j):
-            junk = outp.tile([P, T], F32, name="junk", tag="io", bufs=3)
+            junk = work.tile([P, T], BF16, name="junk", tag="junk", bufs=1)
             nc.scalar.activation(
                 out=junk[:], in_=y[b][:, j, :], func=ACT.Identity, scale=1.0 / T,
                 accum_out=sum_s[:, b, j : j + 1],
@@ -124,8 +153,11 @@ def tile_crosschannelinterp_kernel(tc, x, W, out):
             nc.vector.tensor_tensor(out=pair[:], in0=u[b][:, 0:2, t0 : t0 + TC], in1=u[b][:, 2:4, t0 : t0 + TC], op=ALU.max)
             m4 = work.tile([P, TC], BF16, name="m4", tag="m4")
             nc.vector.tensor_tensor(out=m4[:], in0=pair[:, 0, :], in1=pair[:, 1, :], op=ALU.max)
-            m_t = psum.tile([P, 2, P], F32, name="m_t", tag="tp")
-            m4w = m4[:].bitcast(F32)
+            st["m4", k] = m4
+
+        def max_t(k):
+            m_t = psum.tile([P, 2, P], F32, name="m_t", tag="s_b")
+            m4w = st["m4", k][:].bitcast(F32)
             for blk in range(2):
                 nc.tensor.transpose(m_t[:, blk, :], m4w[:, blk * P : (blk + 1) * P], ident[:])
             st["m_t", k] = m_t
@@ -179,9 +211,13 @@ def tile_crosschannelinterp_kernel(tc, x, W, out):
                     )
             st["ym", k] = ym
 
-        def normalise(k):
+        def recip(k):
             rinv = small.tile([P, 4], F32, name="rinv", tag="rinv")
             nc.vector.reciprocal(out=rinv[:], in_=st["ssum", k][:])
+            st["rinv", k] = rinv
+
+        def normalise(k):
+            rinv = st["rinv", k]
             e_t = st["e_t", k]
             for i in range(4):
                 nc.gpsimd.tensor_scalar(
@@ -267,107 +303,80 @@ def tile_crosschannelinterp_kernel(tc, x, W, out):
             io = outp.tile([P, T], F32, name="io", tag="io", bufs=3)
             nc.scalar.activation(out=io[:], in_=u[b][:, j, :], func=ACT.Exp)
             nc.sync.dma_start(out=out_rows(1, b)[:, j, :], in_=io[:])
+            if len(later) > 1:
+                next_load()
 
-        for k in range(-3, NK + 1):
-            if k == -1:
-                mean_finish(0)
-            if ok(k):
-                product(k, 0)
-            if k == 6:
-                intensity()
-            if ok(k):
-                back(k, 2)
-            if ok(k + 2):
-                exps(k + 2)
+        max_j(0)
+        max_t(0)
+        max_p(0)
+        u_t(0, 0)
+        u_t(0, 1)
+        exps(0)
+        max_j(1)
+        max_t(1)
+        max_j(2)
+        max_p(1)
+        max_t(2)
+        recip(0)
+        normalise(0)
+        max_p(2)
+        for n_ in range(HEAD_FILL):
+            intensity()
+        u_t(1, 0)
+        u_t(1, 1)
+        for j in range(PACK):
+            mean_vector(0, j)
+        mean_finish(0)
+        centre(0, True)
+        group_w()
+        quantise_w()
+        back(0, 0)
+        back(0, 1)
+        for k in range(NK):
+            if ok(k + 1):
+                exps(k + 1)
+                centre(k + 1, False)
+            product(k, 0)
+            back(k, 2)
+            product(k, 1)
+            back(k, 3)
+            product(k, 2)
+            product(k, 3)
+            quantise(k)
+            for jb in (2, 0, 3, 1):
+                multiply(k, jb)
+            if ok(k + 1):
+                recip(k + 1)
+                normalise(k + 1)
             if ok(k + 3):
                 max_j(k + 3)
-            if k == 0:
+                max_t(k + 3)
+            for n_ in range(FILL.get(k, 0)):
                 intensity()
-            if ok(k - 1):
-                representation(k - 1, 0)
-            if k == 1:
-                mean_scalar(1, 0)
-            if k == 4:
-                intensity()
-            if ok(k):
-                product(k, 1)
-            if k == -2:
-                mean_scalar(0, 2)
-            if ok(k - 1):
-                residual(k - 1, 0)
-            if k == 3:
-                intensity()
-            if ok(k):
-                back(k, 3)
-            if k == -1:
-                centre(0, True)
-            if k == 3:
-                intensity()
-            if ok(k):
-                product(k, 2)
-            if k == -2:
-                mean_vector(0, 3)
-            if ok(k - 1):
-                representation(k - 1, 2)
-            if k == 0:
-                quantise_w()
+            for j in MEAN1.get(k, ()):
+                mean_scalar(1, j)
+            for j in MEAN1V.get(k, ()):
+                mean_vector(1, j)
+            if k == 2:
+                mean_finish(1)
+            if ok(k + 2):
+                u_t(k + 2, 0)
+                u_t(k + 2, 1)
+            if ok(k + 1):
+                back(k + 1, 0)
+            residual(k, 2)
+            representation(k, 0)
+            residual(k, 3)
+            representation(k, 1)
             if ok(k + 3):
                 max_p(k + 3)
             if ok(k + 1):
-                back(k + 1, 0)
-            if ok(k + 3):
-                u_t(k + 3, 0)
-            if ok(k):
-                product(k, 3)
-            if ok(k + 2):
-                normalise(k + 2)
-            if k == -2:
-                group_w()
-            if k == 2:
-                mean_scalar(1, 2)
-            if k == 2:
-                mean_finish(1)
-            if ok(k - 1):
-                representation(k - 1, 1)
-            if ok(k - 1):
-                representation(k - 1, 3)
-            if k == 1:
-                mean_scalar(1, 3)
-            if ok(k):
-                quantise(k)
-            if k == -2:
-                intensity()
-            if ok(k - 1):
-                residual(k - 1, 2)
-            if k == -3:
-                mean_vector(0, 0)
-            if ok(k + 3):
-                u_t(k + 3, 1)
-            if ok(k - 1):
-                residual(k - 1, 1)
-            if ok(k - 1):
-                store_representation(k - 1)
-            if k == 5:
-                intensity()
-            if ok(k):
-                multiply(k, 0)
-            if k == 6:
-                intensity()
-            if ok(k - 1):
-                residual(k - 1, 3)
-            if ok(k + 2) and k + 2 > 0:
-                centre(k + 2, False)
-            if ok(k + 1):
                 back(k + 1, 1)
-            if ok(k):
-                multiply(k, 2)
-            if ok(k):
-                multiply(k, 1)
-            if ok(k):
-                multiply(k, 3)
-            if ok(k - 1):
-                store_residual(k - 1)
-            if k == -3:
-                mean_scalar(0, 1)
-            if k == 0:
-                mean_vector(1, 1)
+            residual(k, 0)
+            representation(k, 2)
+            residual(k, 1)
+            representation(k, 3)
+            store_representation(k)
+            store_residual(k)
+            if k == Z1_AFTER:
+                next_load()

@@ -22,13 +22,11 @@ T = 2048
 TC = 512
 NCH = T // TC
 NK = B * NCH
-FILL = {0: 1, 3: 1, 4: 1, 5: 1, 6: 1}
-HEAD_FILL = 3
 Z1_AFTER = 1
-MEAN1 = {1: (0,), 2: (1,)}
-MEAN1V = {1: (2,), 2: (3,)}
-LOADS0 = ("u0a", "u0b", "y0a", "y0b", "W", "z0")
-LOADS1 = ("u1", "y1", "z1")
+S_FILL = {-1: ("I", "I"), 0: ("I", "I"), 1: (0,), 2: (1,), 3: ("I",), 4: ("I",), 5: ("I",), 6: ("I",)}
+V_FILL = {1: (2,), 2: (3,)}
+LOADS0 = ("u0a", "y0a", "y0b", "u0b", "W", "z0", "u1")
+LOADS1 = ("y1", "z1")
 
 
 def tile_crosschannelinterp_kernel(tc, x, W, out):
@@ -58,10 +56,6 @@ def tile_crosschannelinterp_kernel(tc, x, W, out):
                 nc.sync.dma_start(out=u[0][:, :, 0:TC], in_=rows(1, 0)[:, :, 0:TC])
             if name == "u0b":
                 nc.sync.dma_start(out=u[0][:, :, TC:T], in_=rows(1, 0)[:, :, TC:T])
-            if name == "u0c1":
-                nc.sync.dma_start(out=u[0][:, :, TC:2*TC], in_=rows(1, 0)[:, :, TC:2*TC])
-            if name == "u0c23":
-                nc.sync.dma_start(out=u[0][:, :, 2*TC:T], in_=rows(1, 0)[:, :, 2*TC:T])
             if name == "y0a":
                 nc.sync.dma_start(out=y[0][:, 0:2, :], in_=rows(0, 0)[:, 0:2, :])
             if name == "y0b":
@@ -96,10 +90,7 @@ def tile_crosschannelinterp_kernel(tc, x, W, out):
         w_scales = const.tile([P, D], U8, name="w_scales", align_bytes=64)
 
         def group_w():
-            nc.gpsimd.tensor_scalar(
-                out=w_grouped[:], in0=w_raw[:].rearrange("p i (m jb) -> p jb m i", jb=PACK),
-                scalar1=1.0, scalar2=0.0, op0=ALU.mult, op1=ALU.add,
-            )
+            nc.scalar.copy(out=w_grouped[:], in_=w_raw[:].rearrange("p i (m jb) -> p jb m i", jb=PACK))
 
         def quantise_w():
             nc.vector.quantize_mx(
@@ -151,12 +142,16 @@ def tile_crosschannelinterp_kernel(tc, x, W, out):
             b, t0 = where(k)
             pair = work.tile([P, 2, TC], BF16, name="pair", tag="pair")
             nc.vector.tensor_tensor(out=pair[:], in0=u[b][:, 0:2, t0 : t0 + TC], in1=u[b][:, 2:4, t0 : t0 + TC], op=ALU.max)
+            st["pair", k] = pair
+
+        def max_j2(k):
+            pair = st["pair", k]
             m4 = work.tile([P, TC], BF16, name="m4", tag="m4")
             nc.vector.tensor_tensor(out=m4[:], in0=pair[:, 0, :], in1=pair[:, 1, :], op=ALU.max)
             st["m4", k] = m4
 
         def max_t(k):
-            m_t = psum.tile([P, 2, P], F32, name="m_t", tag="s_b")
+            m_t = psum.tile([P, 2, P], F32, name="m_t", tag="tp")
             m4w = st["m4", k][:].bitcast(F32)
             for blk in range(2):
                 nc.tensor.transpose(m_t[:, blk, :], m4w[:, blk * P : (blk + 1) * P], ident[:])
@@ -195,14 +190,14 @@ def tile_crosschannelinterp_kernel(tc, x, W, out):
             st["e_t", k] = e_t
             st["ssum", k] = ssum
 
-        def centre(k, on_vector):
+        def centre(k, on_scalar):
             b, t0 = where(k)
             ym = work.tile([P, PACK, TC], F32, name="ym", tag="ym")
             for j in range(PACK):
-                if on_vector:
-                    nc.vector.tensor_scalar(
-                        out=ym[:, j, :], in0=y[b][:, j, t0 : t0 + TC],
-                        scalar1=negmean[b][:, j : j + 1], scalar2=None, op0=ALU.add,
+                if on_scalar:
+                    nc.scalar.activation(
+                        out=ym[:, j, :], in_=y[b][:, j, t0 : t0 + TC], func=ACT.Identity,
+                        bias=negmean[b][:, j : j + 1], scale=1.0,
                     )
                 else:
                     nc.gpsimd.tensor_scalar(
@@ -291,6 +286,10 @@ def tile_crosschannelinterp_kernel(tc, x, W, out):
                 func=ACT.Identity, bias=mean[b][:, jb : jb + 1], scale=1.0,
             )
 
+        def store_part(k, jb, block, name):
+            b, t0 = where(k)
+            nc.sync.dma_start(out=out_rows(block, b)[:, jb, t0 : t0 + TC], in_=st[name, k][:, jb, :])
+
         def store_representation(k):
             b, t0 = where(k)
             nc.sync.dma_start(out=out_rows(0, b)[:, :, t0 : t0 + TC], in_=st["rep", k][:])
@@ -306,77 +305,82 @@ def tile_crosschannelinterp_kernel(tc, x, W, out):
             if len(later) > 1:
                 next_load()
 
-        max_j(0)
-        max_t(0)
-        max_p(0)
-        u_t(0, 0)
-        u_t(0, 1)
-        exps(0)
-        max_j(1)
-        max_t(1)
-        max_j(2)
-        max_p(1)
-        max_t(2)
-        recip(0)
-        normalise(0)
-        max_p(2)
-        for n_ in range(HEAD_FILL):
-            intensity()
-        u_t(1, 0)
-        u_t(1, 1)
-        for j in range(PACK):
-            mean_vector(0, j)
-        mean_finish(0)
-        centre(0, True)
-        group_w()
-        quantise_w()
-        back(0, 0)
-        back(0, 1)
-        for k in range(NK):
-            if ok(k + 1):
-                exps(k + 1)
-                centre(k + 1, False)
-            product(k, 0)
-            back(k, 2)
-            product(k, 1)
-            back(k, 3)
-            product(k, 2)
-            product(k, 3)
-            quantise(k)
-            for jb in (2, 0, 3, 1):
-                multiply(k, jb)
-            if ok(k + 1):
-                recip(k + 1)
-                normalise(k + 1)
-            if ok(k + 3):
-                max_j(k + 3)
-                max_t(k + 3)
-            for n_ in range(FILL.get(k, 0)):
-                intensity()
-            for j in MEAN1.get(k, ()):
-                mean_scalar(1, j)
-            for j in MEAN1V.get(k, ()):
-                mean_vector(1, j)
-            if k == 2:
-                mean_finish(1)
+        def fill(ops, on_scalar):
+            for op in ops:
+                if op == "I":
+                    intensity()
+                elif on_scalar:
+                    mean_scalar(1, op)
+                else:
+                    mean_vector(1, op)
+
+        def leave(k, q):
+            residual(k, q)
+            if k == NK - 1:
+                store_part(k, q, 2, "ytr")
+
+        for k in range(-4, NK + 1):
+            last = k - 1 == NK - 1
             if ok(k + 2):
-                u_t(k + 2, 0)
-                u_t(k + 2, 1)
-            if ok(k + 1):
-                back(k + 1, 0)
-            residual(k, 2)
-            representation(k, 0)
-            residual(k, 3)
-            representation(k, 1)
+                exps(k + 2)
+            if ok(k):
+                product(k, 0)
+                back(k, 2)
+            if ok(k + 3):
+                max_t(k + 3)
+                u_t(k + 3, 0)
+            if ok(k - 1):
+                leave(k - 1, 0)
+            if ok(k):
+                product(k, 1)
+                back(k, 3)
+            if ok(k - 1):
+                leave(k - 1, 1)
+                for jb in (2, 3, 0, 1):
+                    representation(k - 1, jb)
+                    if last:
+                        store_part(k - 1, jb, 0, "rep")
+                if not last:
+                    store_representation(k - 1)
             if ok(k + 3):
                 max_p(k + 3)
+                u_t(k + 3, 1)
+            if k == -3:
+                for j in range(PACK):
+                    mean_vector(0, j)
+                mean_finish(0)
+            if ok(k):
+                product(k, 2)
+            if ok(k + 1):
+                back(k + 1, 0)
+            if ok(k - 1):
+                leave(k - 1, 2)
+            if ok(k):
+                product(k, 3)
             if ok(k + 1):
                 back(k + 1, 1)
-            residual(k, 0)
-            representation(k, 2)
-            residual(k, 1)
-            representation(k, 3)
-            store_representation(k)
-            store_residual(k)
-            if k == Z1_AFTER:
+            if ok(k - 1):
+                leave(k - 1, 3)
+                if not last:
+                    store_residual(k - 1)
+            if k - 1 == Z1_AFTER:
                 next_load()
+            fill(V_FILL.get(k, ()), False)
+            fill(S_FILL.get(k, ()), True)
+            if k == -2:
+                group_w()
+            if k == 2:
+                mean_finish(1)
+            if ok(k + 4):
+                max_j(k + 4)
+                max_j2(k + 4)
+            if k == -1:
+                quantise_w()
+            if ok(k):
+                quantise(k)
+                for jb in range(4):
+                    multiply(k, jb)
+            if ok(k + 2):
+                recip(k + 2)
+                normalise(k + 2)
+                centre(k + 2, False)

@@ -22,8 +22,8 @@ T = 2048
 TC = 512
 NCH = T // TC
 NK = B * NCH
-Z1_AFTER = 1
-S_FILL = {-1: ("I", "I"), 0: ("I", "I"), 1: (0,), 2: (1,), 3: ("I",), 4: ("I",), 5: ("I",), 6: ("I",)}
+Z1_AFTER = 0
+S_FILL = {-1: ("I", "I"), 0: ("I",), 1: (0, "I"), 2: (1, "I"), 3: ("I",), 4: ("I",), 5: ("I",)}
 V_FILL = {1: (2,), 2: (3,)}
 LOADS0 = ("u0a", "y0a", "y0b", "u0b", "W", "z0", "u1")
 LOADS1 = ("y1", "z1")
@@ -151,7 +151,10 @@ def tile_crosschannelinterp_kernel(tc, x, W, out):
             st["m4", k] = m4
 
         def max_t(k):
-            m_t = psum.tile([P, 2, P], F32, name="m_t", tag="tp")
+            if k in (2, 3):
+                m_t = psum.tile([P, 2, P], F32, name="m_t", tag="acc", bufs=4)
+            else:
+                m_t = psum.tile([P, 2, P], F32, name="m_t", tag="tp")
             m4w = st["m4", k][:].bitcast(F32)
             for blk in range(2):
                 nc.tensor.transpose(m_t[:, blk, :], m4w[:, blk * P : (blk + 1) * P], ident[:])
@@ -169,7 +172,10 @@ def tile_crosschannelinterp_kernel(tc, x, W, out):
         def u_t(k, blk):
             b, t0 = where(k)
             u32 = u[b][:].bitcast(F32)
-            t_u = psum.tile([P, PACK, P], F32, name="t_u", tag="tp")
+            if k == 2:
+                t_u = psum.tile([P, PACK, P], F32, name="t_u", tag="acc", bufs=4)
+            else:
+                t_u = psum.tile([P, PACK, P], F32, name="t_u", tag="tp")
             w0 = t0 // 2 + blk * P
             for j in range(PACK):
                 nc.tensor.transpose(t_u[:, j, :], u32[:, j, w0 : w0 + P], ident[:])
@@ -321,7 +327,7 @@ def tile_crosschannelinterp_kernel(tc, x, W, out):
 
         for k in range(-4, NK + 1):
             last = k - 1 == NK - 1
-            if ok(k + 2):
+            if ok(k + 2) and k + 2 > 0:
                 exps(k + 2)
             if ok(k):
                 product(k, 0)
@@ -346,9 +352,15 @@ def tile_crosschannelinterp_kernel(tc, x, W, out):
                 max_p(k + 3)
                 u_t(k + 3, 1)
             if k == -3:
-                for j in range(PACK):
-                    mean_vector(0, j)
+                exps(0)
+                mean_vector(0, 0)
+                mean_vector(0, 1)
+                recip(0)
+                normalise(0)
+                mean_vector(0, 2)
+                mean_vector(0, 3)
                 mean_finish(0)
+                centre(0, False)
             if ok(k):
                 product(k, 2)
             if ok(k + 1):
@@ -380,7 +392,7 @@ def tile_crosschannelinterp_kernel(tc, x, W, out):
                 quantise(k)
                 for jb in range(4):
                     multiply(k, jb)
-            if ok(k + 2):
+            if ok(k + 2) and k + 2 > 0:
                 recip(k + 2)
                 normalise(k + 2)
                 centre(k + 2, False)

@@ -23,9 +23,9 @@ TC = 512
 NCH = T // TC
 NK = B * NCH
 Z1_AFTER = 0
-S_FILL = {-1: ("I", "I"), 0: ("I",), 1: (0, "I"), 2: (1, "I"), 3: ("I",), 4: ("I",), 5: ("I",)}
+S_FILL = {0: ("I",), 1: (0, "I"), 2: (1, "I"), 3: ("I",), 4: ("I",), 5: ("I",)}
 V_FILL = {1: (2,), 2: (3,)}
-LOADS0 = ("u0a", "y0a", "y0b", "u0b", "W", "z0", "u1")
+LOADS0 = ("u0a", "u0b", "y0a", "y0b", "W", "z0", "u1")
 LOADS1 = ("y1", "z1")
 
 
@@ -46,16 +46,26 @@ def tile_crosschannelinterp_kernel(tc, x, W, out):
         def out_rows(block, b):
             return out[b, block * D : (block + 1) * D, :].rearrange("(p j) t -> p j t", j=PACK)
 
-        u = [const.tile([P, PACK, T], BF16, name="u%d" % b) for b in range(B)]
+        u_first = const.tile([P, PACK, TC], BF16, name="u_first")
+        u_rest = const.tile([P, PACK, T - TC], BF16, name="u_rest")
+        u_second = const.tile([P, PACK, T], BF16, name="u_second")
+
+        def u_chunk(k):
+            if k == 0:
+                return u_first[:]
+            if k < NCH:
+                return u_rest[:, :, (k - 1) * TC : k * TC]
+            return u_second[:, :, (k - NCH) * TC : (k - NCH + 1) * TC]
+
         y = [const.tile([P, PACK, T], BF16, name="y%d" % b) for b in range(B)]
         z = [const.tile([P, PACK, T], BF16, name="z%d" % b) for b in range(B)]
         w_raw = const.tile([P, PACK, D], BF16, name="w_raw")
 
         def load(name):
             if name == "u0a":
-                nc.sync.dma_start(out=u[0][:, :, 0:TC], in_=rows(1, 0)[:, :, 0:TC])
+                nc.sync.dma_start(out=u_first[:], in_=rows(1, 0)[:, :, 0:TC])
             if name == "u0b":
-                nc.sync.dma_start(out=u[0][:, :, TC:T], in_=rows(1, 0)[:, :, TC:T])
+                nc.sync.dma_start(out=u_rest[:], in_=rows(1, 0)[:, :, TC:T])
             if name == "y0a":
                 nc.sync.dma_start(out=y[0][:, 0:2, :], in_=rows(0, 0)[:, 0:2, :])
             if name == "y0b":
@@ -65,7 +75,7 @@ def tile_crosschannelinterp_kernel(tc, x, W, out):
             if name == "z0":
                 nc.sync.dma_start(out=z[0][:], in_=rows(2, 0))
             if name == "u1":
-                nc.sync.dma_start(out=u[1][:], in_=rows(1, 1))
+                nc.sync.dma_start(out=u_second[:], in_=rows(1, 1))
             if name == "y1":
                 nc.sync.dma_start(out=y[1][:], in_=rows(0, 1))
             if name == "z1":
@@ -141,7 +151,7 @@ def tile_crosschannelinterp_kernel(tc, x, W, out):
         def max_j(k):
             b, t0 = where(k)
             pair = work.tile([P, 2, TC], BF16, name="pair", tag="pair")
-            nc.vector.tensor_tensor(out=pair[:], in0=u[b][:, 0:2, t0 : t0 + TC], in1=u[b][:, 2:4, t0 : t0 + TC], op=ALU.max)
+            nc.vector.tensor_tensor(out=pair[:], in0=u_chunk(k)[:, 0:2, :], in1=u_chunk(k)[:, 2:4, :], op=ALU.max)
             st["pair", k] = pair
 
         def max_j2(k):
@@ -151,7 +161,7 @@ def tile_crosschannelinterp_kernel(tc, x, W, out):
             st["m4", k] = m4
 
         def max_t(k):
-            if k in (2, 3):
+            if k < NCH:
                 m_t = psum.tile([P, 2, P], F32, name="m_t", tag="acc", bufs=4)
             else:
                 m_t = psum.tile([P, 2, P], F32, name="m_t", tag="tp")
@@ -171,12 +181,9 @@ def tile_crosschannelinterp_kernel(tc, x, W, out):
 
         def u_t(k, blk):
             b, t0 = where(k)
-            u32 = u[b][:].bitcast(F32)
-            if k == 2:
-                t_u = psum.tile([P, PACK, P], F32, name="t_u", tag="acc", bufs=4)
-            else:
-                t_u = psum.tile([P, PACK, P], F32, name="t_u", tag="tp")
-            w0 = t0 // 2 + blk * P
+            u32 = u_chunk(k).bitcast(F32)
+            t_u = psum.tile([P, PACK, P], F32, name="t_u", tag="tp")
+            w0 = blk * P
             for j in range(PACK):
                 nc.tensor.transpose(t_u[:, j, :], u32[:, j, w0 : w0 + P], ident[:])
             st["t_u", k, blk] = t_u
@@ -306,7 +313,11 @@ def tile_crosschannelinterp_kernel(tc, x, W, out):
             b, j = divmod(todo[0], PACK)
             todo[:1] = []
             io = outp.tile([P, T], F32, name="io", tag="io", bufs=3)
-            nc.scalar.activation(out=io[:], in_=u[b][:, j, :], func=ACT.Exp)
+            if b == 0:
+                nc.scalar.activation(out=io[:, 0:TC], in_=u_first[:, j, :], func=ACT.Exp)
+                nc.scalar.activation(out=io[:, TC:T], in_=u_rest[:, j, :], func=ACT.Exp)
+            else:
+                nc.scalar.activation(out=io[:], in_=u_second[:, j, :], func=ACT.Exp)
             nc.sync.dma_start(out=out_rows(1, b)[:, j, :], in_=io[:])
             if len(later) > 1:
                 next_load()
@@ -325,7 +336,44 @@ def tile_crosschannelinterp_kernel(tc, x, W, out):
             if k == NK - 1:
                 store_part(k, q, 2, "ytr")
 
-        for k in range(-4, NK + 1):
+        max_j(0)
+        max_j2(0)
+        max_t(0)
+        u_t(0, 0)
+        max_p(0)
+        u_t(0, 1)
+        exps(0)
+        max_j(1)
+        max_j2(1)
+        max_t(1)
+        u_t(1, 0)
+        max_p(1)
+        u_t(1, 1)
+        intensity()
+        recip(0)
+        normalise(0)
+        exps(1)
+        for j in range(PACK):
+            mean_vector(0, j)
+        mean_finish(0)
+        centre(0, False)
+        intensity()
+        recip(1)
+        normalise(1)
+        centre(1, False)
+        max_j(2)
+        max_j2(2)
+        max_t(2)
+        u_t(2, 0)
+        max_p(2)
+        u_t(2, 1)
+        group_w()
+        max_j(3)
+        max_j2(3)
+        quantise_w()
+        back(0, 0)
+        back(0, 1)
+        for k in range(NK + 1):
             last = k - 1 == NK - 1
             if ok(k + 2) and k + 2 > 0:
                 exps(k + 2)
@@ -351,16 +399,6 @@ def tile_crosschannelinterp_kernel(tc, x, W, out):
             if ok(k + 3):
                 max_p(k + 3)
                 u_t(k + 3, 1)
-            if k == -3:
-                exps(0)
-                mean_vector(0, 0)
-                mean_vector(0, 1)
-                recip(0)
-                normalise(0)
-                mean_vector(0, 2)
-                mean_vector(0, 3)
-                mean_finish(0)
-                centre(0, False)
             if ok(k):
                 product(k, 2)
             if ok(k + 1):
@@ -379,15 +417,11 @@ def tile_crosschannelinterp_kernel(tc, x, W, out):
                 next_load()
             fill(V_FILL.get(k, ()), False)
             fill(S_FILL.get(k, ()), True)
-            if k == -2:
-                group_w()
             if k == 2:
                 mean_finish(1)
             if ok(k + 4):
                 max_j(k + 4)
                 max_j2(k + 4)
-            if k == -1:
-                quantise_w()
             if ok(k):
                 quantise(k)
                 for jb in range(4):

@@ -23,6 +23,7 @@ TC = 512
 NCH = T // TC
 NK = B * NCH
 Z1_AFTER = 0
+FINE = 6
 S_FILL = {0: ("I",), 1: (0, "I"), 2: (1, "I"), 3: ("I",), 4: ("I",), 5: ("I",)}
 V_FILL = {1: (2,), 2: (3,)}
 LOADS0 = ("u0a", "u0b", "y0a", "y0b", "W", "z0", "u1")
@@ -333,7 +334,7 @@ def tile_crosschannelinterp_kernel(tc, x, W, out):
 
         def leave(k, q):
             residual(k, q)
-            if k == NK - 1:
+            if k >= FINE:
                 store_part(k, q, 2, "ytr")
 
         max_j(0)
@@ -347,6 +348,9 @@ def tile_crosschannelinterp_kernel(tc, x, W, out):
         max_j2(1)
         max_t(1)
         u_t(1, 0)
+        max_j(2)
+        max_j2(2)
+        max_t(2)
         max_p(1)
         u_t(1, 1)
         intensity()
@@ -358,14 +362,11 @@ def tile_crosschannelinterp_kernel(tc, x, W, out):
         mean_finish(0)
         centre(0, False)
         intensity()
+        max_p(2)
         recip(1)
         normalise(1)
         centre(1, False)
-        max_j(2)
-        max_j2(2)
-        max_t(2)
         u_t(2, 0)
-        max_p(2)
         u_t(2, 1)
         group_w()
         max_j(3)
@@ -374,7 +375,7 @@ def tile_crosschannelinterp_kernel(tc, x, W, out):
         back(0, 0)
         back(0, 1)
         for k in range(NK + 1):
-            last = k - 1 == NK - 1
+            last = k - 1 >= FINE
             if ok(k + 2) and k + 2 > 0:
                 exps(k + 2)
             if ok(k):
@@ -383,12 +384,11 @@ def tile_crosschannelinterp_kernel(tc, x, W, out):
             if ok(k + 3):
                 max_t(k + 3)
                 u_t(k + 3, 0)
-            if ok(k - 1):
-                leave(k - 1, 0)
             if ok(k):
                 product(k, 1)
                 back(k, 3)
             if ok(k - 1):
+                leave(k - 1, 0)
                 leave(k - 1, 1)
                 for jb in (2, 3, 0, 1):
                     representation(k - 1, jb)
@@ -396,20 +396,20 @@ def tile_crosschannelinterp_kernel(tc, x, W, out):
                         store_part(k - 1, jb, 0, "rep")
                 if not last:
                     store_representation(k - 1)
-            if ok(k + 3):
-                max_p(k + 3)
-                u_t(k + 3, 1)
             if ok(k):
                 product(k, 2)
             if ok(k + 1):
                 back(k + 1, 0)
-            if ok(k - 1):
+            if ok(k - 1) and k < NK - 1:
                 leave(k - 1, 2)
+            if ok(k + 3):
+                max_p(k + 3)
+                u_t(k + 3, 1)
             if ok(k):
                 product(k, 3)
             if ok(k + 1):
                 back(k + 1, 1)
-            if ok(k - 1):
+            if ok(k - 1) and k < NK - 1:
                 leave(k - 1, 3)
                 if not last:
                     store_residual(k - 1)
@@ -424,6 +424,10 @@ def tile_crosschannelinterp_kernel(tc, x, W, out):
                 max_j2(k + 4)
             if ok(k):
                 quantise(k)
+            if ok(k - 1) and k >= NK - 1:
+                leave(k - 1, 2)
+                leave(k - 1, 3)
+            if ok(k):
                 for jb in range(4):
                     multiply(k, jb)
             if ok(k + 2) and k + 2 > 0:

@@ -23,7 +23,7 @@ TC = 512
 NCH = T // TC
 NK = B * NCH
 Z1_AFTER = 0
-FINE = 6
+FINE = 0
 S_FILL = {0: ("I",), 1: (0, "I"), 2: (1, "I"), 3: ("I",), 4: ("I",), 5: ("I",)}
 V_FILL = {1: (2,), 2: (3,)}
 LOADS0 = ("u0a", "u0b", "y0a", "y0b", "W", "z0", "u1")
@@ -209,9 +209,9 @@ def tile_crosschannelinterp_kernel(tc, x, W, out):
             ym = work.tile([P, PACK, TC], F32, name="ym", tag="ym")
             for j in range(PACK):
                 if on_scalar:
-                    nc.scalar.activation(
-                        out=ym[:, j, :], in_=y[b][:, j, t0 : t0 + TC], func=ACT.Identity,
-                        bias=negmean[b][:, j : j + 1], scale=1.0,
+                    nc.vector.tensor_scalar(
+                        out=ym[:, j, :], in0=y[b][:, j, t0 : t0 + TC],
+                        scalar1=negmean[b][:, j : j + 1], scalar2=None, op0=ALU.add,
                     )
                 else:
                     nc.gpsimd.tensor_scalar(
@@ -360,7 +360,7 @@ def tile_crosschannelinterp_kernel(tc, x, W, out):
         for j in range(PACK):
             mean_vector(0, j)
         mean_finish(0)
-        centre(0, False)
+        centre(0, True)
         intensity()
         max_p(2)
         recip(1)

@@ -225,10 +225,10 @@ def tile_crosschannelinterp_kernel(tc, x, W, out):
             nc.vector.reciprocal(out=rinv[:], in_=st["ssum", k][:])
             st["rinv", k] = rinv
 
-        def normalise(k):
+        def normalise(k, quarters=(0, 1, 2, 3)):
             rinv = st["rinv", k]
             e_t = st["e_t", k]
-            for i in range(4):
+            for i in quarters:
                 nc.gpsimd.tensor_scalar(
                     out=e_t[:, i, :, :], in0=e_t[:, i, :, :],
                     scalar1=rinv[:, i : i + 1], scalar2=0.0, op0=ALU.mult, op1=ALU.add,
@@ -371,7 +371,6 @@ def tile_crosschannelinterp_kernel(tc, x, W, out):
         group_w()
         max_j(3)
         max_j2(3)
-        quantise_w()
         back(0, 0)
         back(0, 1)
         for k in range(NK + 1):
@@ -381,38 +380,38 @@ def tile_crosschannelinterp_kernel(tc, x, W, out):
             if ok(k):
                 product(k, 0)
                 back(k, 2)
+                product(k, 1)
+                back(k, 3)
             if ok(k + 3):
                 max_t(k + 3)
                 u_t(k + 3, 0)
-            if ok(k):
-                product(k, 1)
-                back(k, 3)
+            if k == 0:
+                quantise_w()
             if ok(k - 1):
+                representation(k - 1, 3)
+                store_part(k - 1, 3, 0, "rep")
                 leave(k - 1, 0)
                 leave(k - 1, 1)
-                for jb in (2, 3, 0, 1):
+                if k < NK - 1:
+                    leave(k - 1, 2)
+                for jb in (0, 1):
                     representation(k - 1, jb)
-                    if last:
-                        store_part(k - 1, jb, 0, "rep")
-                if not last:
-                    store_representation(k - 1)
+                    store_part(k - 1, jb, 0, "rep")
             if ok(k):
                 product(k, 2)
             if ok(k + 1):
                 back(k + 1, 0)
-            if ok(k - 1) and k < NK - 1:
-                leave(k - 1, 2)
-            if ok(k + 3):
-                max_p(k + 3)
-                u_t(k + 3, 1)
             if ok(k):
                 product(k, 3)
             if ok(k + 1):
                 back(k + 1, 1)
+            if ok(k + 3):
+                max_p(k + 3)
+                u_t(k + 3, 1)
             if ok(k - 1) and k < NK - 1:
                 leave(k - 1, 3)
-                if not last:
-                    store_residual(k - 1)
+                representation(k - 1, 2)
+                store_part(k - 1, 2, 0, "rep")
             if k - 1 == Z1_AFTER:
                 next_load()
             fill(V_FILL.get(k, ()), False)
@@ -426,11 +425,14 @@ def tile_crosschannelinterp_kernel(tc, x, W, out):
                 quantise(k)
             if ok(k - 1) and k >= NK - 1:
                 leave(k - 1, 2)
+                representation(k - 1, 2)
+                store_part(k - 1, 2, 0, "rep")
                 leave(k - 1, 3)
             if ok(k):
                 for jb in range(4):
                     multiply(k, jb)
             if ok(k + 2) and k + 2 > 0:
                 recip(k + 2)
-                normalise(k + 2)
+                normalise(k + 2, (0, 1))
                 centre(k + 2, False)
+                normalise(k + 2, (2, 3))

@@ -204,11 +204,16 @@ def tile_crosschannelinterp_kernel(tc, x, W, out):
             st["e_t", k] = e_t
             st["ssum", k] = ssum
 
-        def centre(k, on_scalar):
+        def centre(k, on_scalar, n_act=0):
             b, t0 = where(k)
             ym = work.tile([P, PACK, TC], F32, name="ym", tag="ym")
             for j in range(PACK):
-                if on_scalar:
+                if j >= PACK - n_act:
+                    nc.scalar.activation(
+                        out=ym[:, j, :], in_=y[b][:, j, t0 : t0 + TC], func=ACT.Identity,
+                        bias=negmean[b][:, j : j + 1], scale=1.0,
+                    )
+                elif on_scalar:
                     nc.vector.tensor_scalar(
                         out=ym[:, j, :], in0=y[b][:, j, t0 : t0 + TC],
                         scalar1=negmean[b][:, j : j + 1], scalar2=None, op0=ALU.add,
@@ -434,5 +439,5 @@ def tile_crosschannelinterp_kernel(tc, x, W, out):
             if ok(k + 2) and k + 2 > 0:
                 recip(k + 2)
                 normalise(k + 2, (0, 1))
-                centre(k + 2, False)
+                centre(k + 2, False, 1)
                 normalise(k + 2, (2, 3))

@@ -254,8 +254,9 @@ def tile_crosschannelinterp_kernel(tc, x, W, out):
             blk, e = divmod(i, 2)
             n0 = e * 256 + blk * P
             nc.vector.tensor_tensor(
-                out=a_g[:, n0 : n0 + P, :], in0=ymv[:, blk, e, :, :],
-                in1=st["s_b", k, i][:].rearrange("p j w -> p w j"), op=ALU.mult,
+                out=a_g[:, n0 : n0 + P, :].rearrange("p (c i) j -> p c j i", i=4),
+                in0=ymv[:, blk, e, :, :].rearrange("p (c i) j -> p c j i", i=4),
+                in1=st["s_b", k, i][:].rearrange("p j (c i) -> p c j i", i=4), op=ALU.mult,
             )
 
         def quantise(k):

@@ -22,8 +22,9 @@ T = 2048
 TC = 512
 NCH = T // TC
 NK = B * NCH
-Z1_AFTER = 0
+Z1_AFTER = 1
 FINE = 0
+JOINED = ((0, 2, 4), (1, 5))
 S_FILL = {0: ("I",), 1: (0, "I"), 2: (1, "I"), 3: ("I",), 4: ("I",), 5: ("I",)}
 V_FILL = {1: (2,), 2: (3,)}
 LOADS0 = ("u0a", "u0b", "y0a", "y0b", "W", "z0", "u1")
@@ -58,9 +59,14 @@ def tile_crosschannelinterp_kernel(tc, x, W, out):
                 return u_rest[:, :, (k - 1) * TC : k * TC]
             return u_second[:, :, (k - NCH) * TC : (k - NCH + 1) * TC]
 
-        y = [const.tile([P, PACK, T], BF16, name="y%d" % b) for b in range(B)]
-        z = [const.tile([P, PACK, T], BF16, name="z%d" % b) for b in range(B)]
-        w_raw = const.tile([P, PACK, D], BF16, name="w_raw")
+        y = {}
+        z = {}
+
+        def y_or_z():
+            return const.tile([P, PACK, T], BF16, name="y_or_z", tag="y_or_z", bufs=3)
+
+        y[0] = y_or_z()
+        w_raw = outp.tile([P, PACK, D], BF16, name="w_raw", tag="ytr", bufs=8, align_bytes=64)
 
         def load(name):
             if name == "u0a":
@@ -74,12 +80,15 @@ def tile_crosschannelinterp_kernel(tc, x, W, out):
             if name == "W":
                 nc.sync.dma_start(out=w_raw[:], in_=W.rearrange("(p i) j -> p i j", i=PACK))
             if name == "z0":
+                z[0] = y_or_z()
                 nc.sync.dma_start(out=z[0][:], in_=rows(2, 0))
             if name == "u1":
                 nc.sync.dma_start(out=u_second[:], in_=rows(1, 1))
             if name == "y1":
+                y[1] = y_or_z()
                 nc.sync.dma_start(out=y[1][:], in_=rows(0, 1))
             if name == "z1":
+                z[1] = y_or_z()
                 nc.sync.dma_start(out=z[1][:], in_=rows(2, 1))
 
         for name in LOADS0:
@@ -96,7 +105,7 @@ def tile_crosschannelinterp_kernel(tc, x, W, out):
         warm = const.tile([P, 1], F32, name="warm")
         nc.scalar.activation(out=warm[:], in_=ident[:, 0:1], func=ACT.Exp)
 
-        w_grouped = const.tile([P, PACK, P, PACK], BF16, name="w_grouped", align_bytes=64)
+        w_grouped = outp.tile([P, PACK, P, PACK], BF16, name="w_grouped", tag="ytr", bufs=8, align_bytes=64)
         w_codes = const.tile([P, D], U32, name="w_codes", align_bytes=64)
         w_scales = const.tile([P, D], U8, name="w_scales", align_bytes=64)
 
@@ -117,28 +126,22 @@ def tile_crosschannelinterp_kernel(tc, x, W, out):
         nc.vector.memset(sum_s[:], 0.0)
 
         def mean_vector(b, j):
-            junk2 = work.tile([P, T], BF16, name="junk2", tag="junk2", bufs=1)
             nc.vector.tensor_scalar(
-                out=junk2[:], in0=y[b][:, j, :], scalar1=1.0, scalar2=None, op0=ALU.mult, op1=ALU.add,
+                out=y[b][:, j, :], in0=y[b][:, j, :], scalar1=1.0, scalar2=None, op0=ALU.mult, op1=ALU.add,
                 accum_out=sum_v[:, b, j : j + 1],
             )
 
         def mean_scalar(b, j):
-            junk = work.tile([P, T], BF16, name="junk", tag="junk", bufs=1)
             nc.scalar.activation(
-                out=junk[:], in_=y[b][:, j, :], func=ACT.Identity, scale=1.0 / T,
+                out=y[b][:, j, :], in_=y[b][:, j, :], func=ACT.Identity, scale=1.0,
                 accum_out=sum_s[:, b, j : j + 1],
             )
 
         def mean_finish(b):
-            nc.vector.scalar_tensor_tensor(
-                out=negmean[b][:], in0=sum_v[:, b, :], scalar=-1.0 / T, in1=sum_s[:, b, :],
-                op0=ALU.mult, op1=ALU.subtract,
-            )
-            nc.vector.scalar_tensor_tensor(
-                out=mean[b][:], in0=sum_v[:, b, :], scalar=1.0 / T, in1=sum_s[:, b, :],
-                op0=ALU.mult, op1=ALU.add,
-            )
+            total = small.tile([P, PACK], F32, name="total", tag="total")
+            nc.vector.tensor_tensor(out=total[:], in0=sum_v[:, b, :], in1=sum_s[:, b, :], op=ALU.add)
+            nc.vector.tensor_scalar(out=negmean[b][:], in0=total[:], scalar1=-1.0 / T, scalar2=None, op0=ALU.mult)
+            nc.vector.tensor_scalar(out=mean[b][:], in0=total[:], scalar1=1.0 / T, scalar2=None, op0=ALU.mult)
 
         st = {}
 
@@ -280,39 +283,41 @@ def tile_crosschannelinterp_kernel(tc, x, W, out):
             )
             st["acc", k, jb] = acc
 
+        def span(k, jb):
+            for first in JOINED[jb // 2]:
+                if first <= k <= first + 1:
+                    return first, 2
+            return k, 1
+
+        def part(name, k, jb):
+            first, n = span(k, jb)
+            if k == first:
+                st[name, first, jb] = outp.tile([P, n * TC], F32, name=name, tag=name, bufs=8, align_bytes=64)
+            return st[name, first, jb][:, (k - first) * TC : (k - first + 1) * TC]
+
         def residual(k, jb):
             b, t0 = where(k)
-            if st.get(("ytr", k)) is None:
-                st["ytr", k] = outp.tile([P, PACK, TC], F32, name="ytr", tag="ytr")
             nc.vector.scalar_tensor_tensor(
-                out=st["ytr", k][:, jb, :].rearrange("m (w e) -> m w e", e=2),
+                out=part("ytr", k, jb).rearrange("m (w e) -> m w e", e=2),
                 in0=z[b][:, jb, t0 : t0 + TC].rearrange("m (w e) -> m w e", e=2),
                 scalar=mean[b][:, jb : jb + 1],
                 in1=st["acc", k, jb][:].rearrange("m (e w) -> m w e", e=2),
                 op0=ALU.subtract, op1=ALU.subtract,
             )
 
-        def store_residual(k):
-            b, t0 = where(k)
-            nc.sync.dma_start(out=out_rows(2, b)[:, :, t0 : t0 + TC], in_=st["ytr", k][:])
-
         def representation(k, jb):
             b, t0 = where(k)
-            if st.get(("rep", k)) is None:
-                st["rep", k] = outp.tile([P, PACK, TC], F32, name="rep", tag="rep")
             nc.scalar.activation(
-                out=st["rep", k][:, jb, :].rearrange("m (w e) -> m w e", e=2),
+                out=part("rep", k, jb).rearrange("m (w e) -> m w e", e=2),
                 in_=st["acc", k, jb][:].rearrange("m (e w) -> m w e", e=2),
                 func=ACT.Identity, bias=mean[b][:, jb : jb + 1], scale=1.0,
             )
 
         def store_part(k, jb, block, name):
-            b, t0 = where(k)
-            nc.sync.dma_start(out=out_rows(block, b)[:, jb, t0 : t0 + TC], in_=st[name, k][:, jb, :])
-
-        def store_representation(k):
-            b, t0 = where(k)
-            nc.sync.dma_start(out=out_rows(0, b)[:, :, t0 : t0 + TC], in_=st["rep", k][:])
+            first, n = span(k, jb)
+            if k == first + n - 1:
+                b, t0 = where(first)
+                nc.sync.dma_start(out=out_rows(block, b)[:, jb, t0 : t0 + n * TC], in_=st[name, first, jb][:])
 
         todo = list(range(B * PACK))
 

@@ -22,7 +22,7 @@ T = 2048
 TC = 512
 NCH = T // TC
 NK = B * NCH
-Z1_AFTER = 1
+Z1_AFTER = 0
 FINE = 0
 JOINED = ((0, 2, 4), (1, 5))
 S_FILL = {0: ("I",), 1: (0, "I"), 2: (1, "I"), 3: ("I",), 4: ("I",), 5: ("I",)}
@@ -63,10 +63,10 @@ def tile_crosschannelinterp_kernel(tc, x, W, out):
         z = {}
 
         def y_or_z():
-            return const.tile([P, PACK, T], BF16, name="y_or_z", tag="y_or_z", bufs=3)
+            return const.tile([P, PACK, T], BF16, name="y_or_z", tag="y_or_z", bufs=4)
 
         y[0] = y_or_z()
-        w_raw = outp.tile([P, PACK, D], BF16, name="w_raw", tag="ytr", bufs=8, align_bytes=64)
+        w_raw = outp.tile([P, PACK, D], BF16, name="w_raw", tag="ytr", bufs=6, align_bytes=64)
 
         def load(name):
             if name == "u0a":
@@ -105,7 +105,10 @@ def tile_crosschannelinterp_kernel(tc, x, W, out):
         warm = const.tile([P, 1], F32, name="warm")
         nc.scalar.activation(out=warm[:], in_=ident[:, 0:1], func=ACT.Exp)
 
-        w_grouped = outp.tile([P, PACK, P, PACK], BF16, name="w_grouped", tag="ytr", bufs=8, align_bytes=64)
+        w_grouped = outp.tile([P, PACK, P, PACK], BF16, name="w_grouped", tag="ytr", bufs=6, align_bytes=64)
+        ident_bf = const.tile([P, P], BF16, name="ident_bf")
+        make_identity(nc, ident_bf[:])
+        folded_sb = const.tile([P, TC], F32, name="folded_sb")
         w_codes = const.tile([P, D], U32, name="w_codes", align_bytes=64)
         w_scales = const.tile([P, D], U8, name="w_scales", align_bytes=64)
 
@@ -131,9 +134,18 @@ def tile_crosschannelinterp_kernel(tc, x, W, out):
                 accum_out=sum_v[:, b, j : j + 1],
             )
 
+        def fold(b, j):
+            folded = psum.tile([P, TC], F32, name="folded", tag="acc", bufs=4)
+            for q in range(NCH):
+                nc.tensor.matmul(
+                    out=folded[:], lhsT=ident_bf[:], rhs=y[b][:, j, q * TC : (q + 1) * TC],
+                    start=(q == 0), stop=(q == NCH - 1),
+                )
+            st["folded", b, j] = folded
+
         def mean_scalar(b, j):
             nc.scalar.activation(
-                out=y[b][:, j, :], in_=y[b][:, j, :], func=ACT.Identity, scale=1.0,
+                out=folded_sb[:], in_=st["folded", b, j][:], func=ACT.Identity, scale=1.0,
                 accum_out=sum_s[:, b, j : j + 1],
             )
 
@@ -292,7 +304,7 @@ def tile_crosschannelinterp_kernel(tc, x, W, out):
         def part(name, k, jb):
             first, n = span(k, jb)
             if k == first:
-                st[name, first, jb] = outp.tile([P, n * TC], F32, name=name, tag=name, bufs=8, align_bytes=64)
+                st[name, first, jb] = outp.tile([P, n * TC], F32, name=name, tag=name, bufs=6, align_bytes=64)
             return st[name, first, jb][:, (k - first) * TC : (k - first + 1) * TC]
 
         def residual(k, jb):
@@ -320,17 +332,23 @@ def tile_crosschannelinterp_kernel(tc, x, W, out):
                 nc.sync.dma_start(out=out_rows(block, b)[:, jb, t0 : t0 + n * TC], in_=st[name, first, jb][:])
 
         todo = list(range(B * PACK))
+        io = {}
+
+        def intensity_first(j):
+            io[j] = outp.tile([P, T], F32, name="io", tag="io", bufs=3)
+            nc.scalar.activation(out=io[j][:, 0:TC], in_=u_first[:, j, :], func=ACT.Exp)
 
         def intensity():
             b, j = divmod(todo[0], PACK)
             todo[:1] = []
-            io = outp.tile([P, T], F32, name="io", tag="io", bufs=3)
             if b == 0:
-                nc.scalar.activation(out=io[:, 0:TC], in_=u_first[:, j, :], func=ACT.Exp)
-                nc.scalar.activation(out=io[:, TC:T], in_=u_rest[:, j, :], func=ACT.Exp)
+                if j not in io:
+                    intensity_first(j)
+                nc.scalar.activation(out=io[j][:, TC:T], in_=u_rest[:, j, :], func=ACT.Exp)
             else:
-                nc.scalar.activation(out=io[:], in_=u_second[:, j, :], func=ACT.Exp)
-            nc.sync.dma_start(out=out_rows(1, b)[:, j, :], in_=io[:])
+                io[j] = outp.tile([P, T], F32, name="io", tag="io", bufs=3)
+                nc.scalar.activation(out=io[j][:], in_=u_second[:, j, :], func=ACT.Exp)
+            nc.sync.dma_start(out=out_rows(1, b)[:, j, :], in_=io[j][:])
             if len(later) > 1:
                 next_load()
 
@@ -352,6 +370,8 @@ def tile_crosschannelinterp_kernel(tc, x, W, out):
         max_j2(0)
         max_t(0)
         u_t(0, 0)
+        for j in range(3):
+            intensity_first(j)
         max_p(0)
         u_t(0, 1)
         exps(0)
@@ -371,19 +391,19 @@ def tile_crosschannelinterp_kernel(tc, x, W, out):
         for j in range(PACK):
             mean_vector(0, j)
         mean_finish(0)
-        centre(0, True)
-        intensity()
+        centre(0, True, 2)
+        centre(1, False)
         max_p(2)
+        max_j(3)
+        max_j2(3)
         recip(1)
         normalise(1)
-        centre(1, False)
+        back(0, 0)
+        back(0, 1)
         u_t(2, 0)
         u_t(2, 1)
         group_w()
-        max_j(3)
-        max_j2(3)
-        back(0, 0)
-        back(0, 1)
+        intensity()
         for k in range(NK + 1):
             last = k - 1 >= FINE
             if ok(k + 2) and k + 2 > 0:
@@ -408,6 +428,8 @@ def tile_crosschannelinterp_kernel(tc, x, W, out):
                 for jb in (0, 1):
                     representation(k - 1, jb)
                     store_part(k - 1, jb, 0, "rep")
+            if k in (1, 2):
+                fold(1, k - 1)
             if ok(k):
                 product(k, 2)
             if ok(k + 1):
@@ -445,5 +467,5 @@ def tile_crosschannelinterp_kernel(tc, x, W, out):
             if ok(k + 2) and k + 2 > 0:
                 recip(k + 2)
                 normalise(k + 2, (0, 1))
-                centre(k + 2, False, 1)
+                centre(k + 2, False)
                 normalise(k + 2, (2, 3))

@@ -66,7 +66,7 @@ def tile_crosschannelinterp_kernel(tc, x, W, out):
             return const.tile([P, PACK, T], BF16, name="y_or_z", tag="y_or_z", bufs=4)
 
         y[0] = y_or_z()
-        w_raw = outp.tile([P, PACK, D], BF16, name="w_raw", tag="ytr", bufs=6, align_bytes=64)
+        w_raw = outp.tile([P, PACK, D], BF16, name="w_raw", tag="ytr", bufs=8, align_bytes=64)
 
         def load(name):
             if name == "u0a":
@@ -105,7 +105,7 @@ def tile_crosschannelinterp_kernel(tc, x, W, out):
         warm = const.tile([P, 1], F32, name="warm")
         nc.scalar.activation(out=warm[:], in_=ident[:, 0:1], func=ACT.Exp)
 
-        w_grouped = outp.tile([P, PACK, P, PACK], BF16, name="w_grouped", tag="ytr", bufs=6, align_bytes=64)
+        w_grouped = outp.tile([P, PACK, P, PACK], BF16, name="w_grouped", tag="ytr", bufs=8, align_bytes=64)
         ident_bf = const.tile([P, P], BF16, name="ident_bf")
         make_identity(nc, ident_bf[:])
         folded_sb = const.tile([P, TC], F32, name="folded_sb")
@@ -166,7 +166,7 @@ def tile_crosschannelinterp_kernel(tc, x, W, out):
 
         def max_j(k):
             b, t0 = where(k)
-            pair = work.tile([P, 2, TC], BF16, name="pair", tag="pair")
+            pair = work.tile([P, 2, TC], BF16, name="pair", tag="pair", bufs=1)
             nc.vector.tensor_tensor(out=pair[:], in0=u_chunk(k)[:, 0:2, :], in1=u_chunk(k)[:, 2:4, :], op=ALU.max)
             st["pair", k] = pair
 
@@ -219,26 +219,27 @@ def tile_crosschannelinterp_kernel(tc, x, W, out):
             st["e_t", k] = e_t
             st["ssum", k] = ssum
 
-        def centre(k, on_scalar, n_act=0):
+        def centre(k, engines):
             b, t0 = where(k)
-            ym = work.tile([P, PACK, TC], F32, name="ym", tag="ym")
-            for j in range(PACK):
-                if j >= PACK - n_act:
+            if st.get(("ym", k)) is None:
+                st["ym", k] = work.tile([P, PACK, TC], F32, name="ym", tag="ym")
+            ym = st["ym", k]
+            for j, engine in enumerate(engines):
+                if engine == "S":
                     nc.scalar.activation(
                         out=ym[:, j, :], in_=y[b][:, j, t0 : t0 + TC], func=ACT.Identity,
                         bias=negmean[b][:, j : j + 1], scale=1.0,
                     )
-                elif on_scalar:
+                elif engine == "V":
                     nc.vector.tensor_scalar(
                         out=ym[:, j, :], in0=y[b][:, j, t0 : t0 + TC],
                         scalar1=negmean[b][:, j : j + 1], scalar2=None, op0=ALU.add,
                     )
-                else:
+                elif engine == "G":
                     nc.gpsimd.tensor_scalar(
                         out=ym[:, j, :], in0=y[b][:, j, t0 : t0 + TC],
                         scalar1=negmean[b][:, j : j + 1], scalar2=1.0, op0=ALU.add, op1=ALU.mult,
                     )
-            st["ym", k] = ym
 
         def recip(k):
             rinv = small.tile([P, 4], F32, name="rinv", tag="rinv")
@@ -263,7 +264,7 @@ def tile_crosschannelinterp_kernel(tc, x, W, out):
 
         def product(k, i):
             if i == 0:
-                st["a_g", k] = work.tile([P, TC, PACK], BF16, name="a_g", tag="a_g", align_bytes=64)
+                st["a_g", k] = work.tile([P, TC, PACK], BF16, name="a_g", tag="a_g", bufs=1, align_bytes=64)
             a_g = st["a_g", k]
             ymv = st["ym", k][:].rearrange("p j (b w e) -> p b e w j", b=2, e=2)
             blk, e = divmod(i, 2)
@@ -275,8 +276,8 @@ def tile_crosschannelinterp_kernel(tc, x, W, out):
             )
 
         def quantise(k):
-            codes = work.tile([P, TC], U32, name="codes", tag="codes", align_bytes=64)
-            scales = work.tile([P, TC], U8, name="scales", tag="scales", align_bytes=64)
+            codes = work.tile([P, TC], U32, name="codes", tag="codes", bufs=1, align_bytes=64)
+            scales = work.tile([P, TC], U8, name="scales", tag="scales", bufs=1, align_bytes=64)
             nc.vector.quantize_mx(
                 out=codes[:].bitcast(FP8X4), scales=scales[:],
                 in_=st["a_g", k][:].rearrange("p n j -> p (n j)"),
@@ -304,7 +305,7 @@ def tile_crosschannelinterp_kernel(tc, x, W, out):
         def part(name, k, jb):
             first, n = span(k, jb)
             if k == first:
-                st[name, first, jb] = outp.tile([P, n * TC], F32, name=name, tag=name, bufs=6, align_bytes=64)
+                st[name, first, jb] = outp.tile([P, n * TC], F32, name=name, tag=name, bufs=8 if name == "ytr" else 7, align_bytes=64)
             return st[name, first, jb][:, (k - first) * TC : (k - first + 1) * TC]
 
         def residual(k, jb):
@@ -391,13 +392,13 @@ def tile_crosschannelinterp_kernel(tc, x, W, out):
         for j in range(PACK):
             mean_vector(0, j)
         mean_finish(0)
-        centre(0, True, 2)
-        centre(1, False)
+        centre(0, "VVSS")
         max_p(2)
         max_j(3)
         max_j2(3)
         recip(1)
         normalise(1)
+        centre(1, "--GG")
         back(0, 0)
         back(0, 1)
         u_t(2, 0)
@@ -416,8 +417,6 @@ def tile_crosschannelinterp_kernel(tc, x, W, out):
             if ok(k + 3):
                 max_t(k + 3)
                 u_t(k + 3, 0)
-            if k == 0:
-                quantise_w()
             if ok(k - 1):
                 representation(k - 1, 3)
                 store_part(k - 1, 3, 0, "rep")
@@ -454,8 +453,12 @@ def tile_crosschannelinterp_kernel(tc, x, W, out):
             if ok(k + 4):
                 max_j(k + 4)
                 max_j2(k + 4)
+            if k == 0:
+                quantise_w()
             if ok(k):
                 quantise(k)
+            if k == 0:
+                centre(1, "VV--")
             if ok(k - 1) and k >= NK - 1:
                 leave(k - 1, 2)
                 representation(k - 1, 2)
@@ -465,7 +468,8 @@ def tile_crosschannelinterp_kernel(tc, x, W, out):
                 for jb in range(4):
                     multiply(k, jb)
             if ok(k + 2) and k + 2 > 0:
+                centre(k + 2, "VV--")
                 recip(k + 2)
                 normalise(k + 2, (0, 1))
-                centre(k + 2, False)
+                centre(k + 2, "--GS")
                 normalise(k + 2, (2, 3))

@@ -25,7 +25,7 @@ NK = B * NCH
 Z1_AFTER = 0
 FINE = 0
 JOINED = ((0, 2, 4), (1, 5))
-S_FILL = {0: ("I",), 1: (0, "I"), 2: (1, "I"), 3: ("I",), 4: ("I",), 5: ("I",)}
+S_FILL = {0: ("I",), 1: ("I", 0), 2: ("I", 1), 3: ("I",), 4: ("I",), 5: ("I",)}
 V_FILL = {1: (2,), 2: (3,)}
 LOADS0 = ("u0a", "u0b", "y0a", "y0b", "W", "z0", "u1")
 LOADS1 = ("y1", "z1")
@@ -143,6 +143,11 @@ def tile_crosschannelinterp_kernel(tc, x, W, out):
                 )
             st["folded", b, j] = folded
 
+        def mean_folded(b, j):
+            nc.vector.tensor_reduce(
+                out=sum_v[:, b, j : j + 1], in_=st["folded", b, j][:], axis=AX.X, op=ALU.add,
+            )
+
         def mean_scalar(b, j):
             nc.scalar.activation(
                 out=folded_sb[:], in_=st["folded", b, j][:], func=ACT.Identity, scale=1.0,
@@ -150,10 +155,14 @@ def tile_crosschannelinterp_kernel(tc, x, W, out):
             )
 
         def mean_finish(b):
-            total = small.tile([P, PACK], F32, name="total", tag="total")
-            nc.vector.tensor_tensor(out=total[:], in0=sum_v[:, b, :], in1=sum_s[:, b, :], op=ALU.add)
-            nc.vector.tensor_scalar(out=negmean[b][:], in0=total[:], scalar1=-1.0 / T, scalar2=None, op0=ALU.mult)
-            nc.vector.tensor_scalar(out=mean[b][:], in0=total[:], scalar1=1.0 / T, scalar2=None, op0=ALU.mult)
+            if b == 0:
+                total = sum_v[:, b, :]
+            else:
+                total_tile = small.tile([P, PACK], F32, name="total_tile", tag="total_tile")
+                nc.vector.tensor_tensor(out=total_tile[:], in0=sum_v[:, b, :], in1=sum_s[:, b, :], op=ALU.add)
+                total = total_tile[:]
+            nc.vector.tensor_scalar(out=negmean[b][:], in0=total, scalar1=-1.0 / T, scalar2=None, op0=ALU.mult)
+            nc.vector.tensor_scalar(out=mean[b][:], in0=total, scalar1=1.0 / T, scalar2=None, op0=ALU.mult)
 
         st = {}
 
@@ -389,12 +398,15 @@ def tile_crosschannelinterp_kernel(tc, x, W, out):
         recip(0)
         normalise(0)
         exps(1)
-        for j in range(PACK):
+        intensity()
+        fold(0, 3)
+        for j in range(PACK - 1):
             mean_vector(0, j)
-        mean_finish(0)
-        centre(0, "VVSS")
+        mean_folded(0, 3)
         max_p(2)
+        mean_finish(0)
         max_j(3)
+        centre(0, "VVSS")
         max_j2(3)
         recip(1)
         normalise(1)
@@ -404,7 +416,6 @@ def tile_crosschannelinterp_kernel(tc, x, W, out):
         u_t(2, 0)
         u_t(2, 1)
         group_w()
-        intensity()
         for k in range(NK + 1):
             last = k - 1 >= FINE
             if ok(k + 2) and k + 2 > 0:
@@ -448,17 +459,20 @@ def tile_crosschannelinterp_kernel(tc, x, W, out):
                 next_load()
             fill(V_FILL.get(k, ()), False)
             fill(S_FILL.get(k, ()), True)
-            if k == 2:
-                mean_finish(1)
-            if ok(k + 4):
-                max_j(k + 4)
-                max_j2(k + 4)
             if k == 0:
                 quantise_w()
             if ok(k):
                 quantise(k)
             if k == 0:
                 centre(1, "VV--")
+            if ok(k + 4):
+                max_j(k + 4)
+            if k == 2:
+                mean_finish(1)
+            if ok(k + 2) and k + 2 > 0:
+                centre(k + 2, "VV--")
+            if ok(k + 4):
+                max_j2(k + 4)
             if ok(k - 1) and k >= NK - 1:
                 leave(k - 1, 2)
                 representation(k - 1, 2)
@@ -468,8 +482,7 @@ def tile_crosschannelinterp_kernel(tc, x, W, out):
                 for jb in range(4):
                     multiply(k, jb)
             if ok(k + 2) and k + 2 > 0:
-                centre(k + 2, "VV--")
                 recip(k + 2)
                 normalise(k + 2, (0, 1))
-                centre(k + 2, "--GS")
+                centre(k + 2, "--GG")
                 normalise(k + 2, (2, 3))

from contextlib import ExitStack

import concourse.mybir as mybir
from concourse.masks import make_identity

FLOPS = 2 * 2 * 2048 * 512 * 512

F32 = mybir.dt.float32
BF16 = mybir.dt.bfloat16
U32 = mybir.dt.uint32
U8 = mybir.dt.uint8
FP8X4 = mybir.dt.float8_e4m3fn_x4
ALU = mybir.AluOpType
ACT = mybir.ActivationFunctionType
AX = mybir.AxisListType

P = 128
PACK = 4
B = 2
D = 512
T = 2048
TC = 512
NCH = T // TC
NK = B * NCH
Z1_AFTER = 0
FINE = 0
JOINED = ((0, 2, 4), (1, 5))
S_FILL = {0: ("I",), 1: ("I", 0), 2: ("I", 1), 3: ("I",), 4: ("I",), 5: ("I",)}
V_FILL = {1: (2,), 2: (3,)}
LOADS0 = ("u0a", "u0b", "y0a", "y0b", "W", "z0", "u1")
LOADS1 = ("y1", "z1")


def tile_crosschannelinterp_kernel(tc, x, W, out):
    nc = tc.nc
    with ExitStack() as ctx:
        ctx.enter_context(nc.allow_non_contiguous_dma(reason="time chunks of channel rows"))
        const = ctx.enter_context(tc.tile_pool(name="const", bufs=1))
        work = ctx.enter_context(tc.tile_pool(name="work", bufs=2))
        small = ctx.enter_context(tc.tile_pool(name="small", bufs=4))
        outp = ctx.enter_context(tc.tile_pool(name="outp", bufs=2))
        psum = ctx.enter_context(tc.psum_pool(name="psum", bufs=2))
        ctx.enter_context(tc.manual_schedule())

        def rows(block, b):
            return x[b, block * D : (block + 1) * D, :].rearrange("(p j) t -> p j t", j=PACK)

        def out_rows(block, b):
            return out[b, block * D : (block + 1) * D, :].rearrange("(p j) t -> p j t", j=PACK)

        u_first = const.tile([P, PACK, TC], BF16, name="u_first")
        u_rest = const.tile([P, PACK, T - TC], BF16, name="u_rest")
        u_second = const.tile([P, PACK, T], BF16, name="u_second")

        def u_chunk(k):
            if k == 0:
                return u_first[:]
            if k < NCH:
                return u_rest[:, :, (k - 1) * TC : k * TC]
            return u_second[:, :, (k - NCH) * TC : (k - NCH + 1) * TC]

        y = {}
        z = {}

        def y_or_z():
            return const.tile([P, PACK, T], BF16, name="y_or_z", tag="y_or_z", bufs=4)

        y[0] = y_or_z()
        w_raw = outp.tile([P, PACK, D], BF16, name="w_raw", tag="ytr", bufs=8, align_bytes=64)

        def load(name):
            if name == "u0a":
                nc.sync.dma_start(out=u_first[:], in_=rows(1, 0)[:, :, 0:TC])
            if name == "u0b":
                nc.sync.dma_start(out=u_rest[:], in_=rows(1, 0)[:, :, TC:T])
            if name == "y0a":
                nc.sync.dma_start(out=y[0][:, 0:2, :], in_=rows(0, 0)[:, 0:2, :])
            if name == "y0b":
                nc.sync.dma_start(out=y[0][:, 2:4, :], in_=rows(0, 0)[:, 2:4, :])
            if name == "W":
                nc.sync.dma_start(out=w_raw[:], in_=W.rearrange("(p i) j -> p i j", i=PACK))
            if name == "z0":
                z[0] = y_or_z()
                nc.sync.dma_start(out=z[0][:], in_=rows(2, 0))
            if name == "u1":
                nc.sync.dma_start(out=u_second[:], in_=rows(1, 1))
            if name == "y1":
                y[1] = y_or_z()
                nc.sync.dma_start(out=y[1][:], in_=rows(0, 1))
            if name == "z1":
                z[1] = y_or_z()
                nc.sync.dma_start(out=z[1][:], in_=rows(2, 1))

        for name in LOADS0:
            load(name)
        later = list(LOADS1)

        def next_load():
            if later:
                load(later[0])
                later[:1] = []

        ident = const.tile([P, P], F32, name="ident")
        make_identity(nc, ident[:])
        warm = const.tile([P, 1], F32, name="warm")
        nc.scalar.activation(out=warm[:], in_=ident[:, 0:1], func=ACT.Exp)

        w_grouped = outp.tile([P, PACK, P, PACK], BF16, name="w_grouped", tag="ytr", bufs=8, align_bytes=64)
        ident_bf = const.tile([P, P], BF16, name="ident_bf")
        make_identity(nc, ident_bf[:])
        folded_sb = const.tile([P, TC], F32, name="folded_sb")
        w_codes = const.tile([P, D], U32, name="w_codes", align_bytes=64)
        w_scales = const.tile([P, D], U8, name="w_scales", align_bytes=64)

        def group_w():
            nc.scalar.copy(out=w_grouped[:], in_=w_raw[:].rearrange("p i (m jb) -> p jb m i", jb=PACK))

        def quantise_w():
            nc.vector.quantize_mx(
                out=w_codes[:].bitcast(FP8X4), scales=w_scales[:],
                in_=w_grouped[:].rearrange("p jb m i -> p (jb m i)"),
            )

        mean = [const.tile([P, PACK], F32, name="mean%d" % b) for b in range(B)]
        negmean = [const.tile([P, PACK], F32, name="negmean%d" % b) for b in range(B)]
        sum_v = const.tile([P, B, PACK], F32, name="sum_v")
        sum_s = const.tile([P, B, PACK], F32, name="sum_s")
        nc.vector.memset(sum_v[:], 0.0)
        nc.vector.memset(sum_s[:], 0.0)

        def mean_vector(b, j):
            nc.vector.tensor_scalar(
                out=y[b][:, j, :], in0=y[b][:, j, :], scalar1=1.0, scalar2=None, op0=ALU.mult, op1=ALU.add,
                accum_out=sum_v[:, b, j : j + 1],
            )

        def fold(b, j):
            folded = psum.tile([P, TC], F32, name="folded", tag="acc", bufs=4)
            for q in range(NCH):
                nc.tensor.matmul(
                    out=folded[:], lhsT=ident_bf[:], rhs=y[b][:, j, q * TC : (q + 1) * TC],
                    start=(q == 0), stop=(q == NCH - 1),
                )
            st["folded", b, j] = folded

        def mean_folded(b, j):
            nc.vector.tensor_reduce(
                out=sum_v[:, b, j : j + 1], in_=st["folded", b, j][:], axis=AX.X, op=ALU.add,
            )

        def mean_scalar(b, j):
            nc.scalar.activation(
                out=folded_sb[:], in_=st["folded", b, j][:], func=ACT.Identity, scale=1.0,
                accum_out=sum_s[:, b, j : j + 1],
            )

        def mean_finish(b):
            if b == 0:
                total = sum_v[:, b, :]
            else:
                total_tile = small.tile([P, PACK], F32, name="total_tile", tag="total_tile")
                nc.vector.tensor_tensor(out=total_tile[:], in0=sum_v[:, b, :], in1=sum_s[:, b, :], op=ALU.add)
                total = total_tile[:]
            nc.vector.tensor_scalar(out=negmean[b][:], in0=total, scalar1=-1.0 / T, scalar2=None, op0=ALU.mult)
            nc.vector.tensor_scalar(out=mean[b][:], in0=total, scalar1=1.0 / T, scalar2=None, op0=ALU.mult)

        st = {}

        def where(k):
            b, c = divmod(k, NCH)
            return b, c * TC

        def ok(k):
            return 0 <= k < NK

        def max_j(k):
            b, t0 = where(k)
            pair = work.tile([P, 2, TC], BF16, name="pair", tag="pair", bufs=1)
            nc.vector.tensor_tensor(out=pair[:], in0=u_chunk(k)[:, 0:2, :], in1=u_chunk(k)[:, 2:4, :], op=ALU.max)
            st["pair", k] = pair

        def max_j2(k):
            pair = st["pair", k]
            m4 = work.tile([P, TC], BF16, name="m4", tag="m4")
            nc.vector.tensor_tensor(out=m4[:], in0=pair[:, 0, :], in1=pair[:, 1, :], op=ALU.max)
            st["m4", k] = m4

        def max_t(k):
            if k < NCH:
                m_t = psum.tile([P, 2, P], F32, name="m_t", tag="acc", bufs=4)
            else:
                m_t = psum.tile([P, 2, P], F32, name="m_t", tag="tp")
            m4w = st["m4", k][:].bitcast(F32)
            for blk in range(2):
                nc.tensor.transpose(m_t[:, blk, :], m4w[:, blk * P : (blk + 1) * P], ident[:])
            st["m_t", k] = m_t

        def max_p(k):
            negm = small.tile([P, 4], F32, name="negm", tag="negm")
            nc.vector.tensor_reduce(
                out=negm[:].rearrange("w (b e) -> w b e", e=2),
                in_=st["m_t", k][:].bitcast(BF16).rearrange("w b (p e) -> w b e p", e=2),
                axis=AX.X, op=ALU.max, negate=True,
            )
            st["negm", k] = negm

        def u_t(k, blk):
            b, t0 = where(k)
            u32 = u_chunk(k).bitcast(F32)
            t_u = psum.tile([P, PACK, P], F32, name="t_u", tag="tp")
            w0 = blk * P
            for j in range(PACK):
                nc.tensor.transpose(t_u[:, j, :], u32[:, j, w0 : w0 + P], ident[:])
            st["t_u", k, blk] = t_u

        def exps(k):
            negm = st["negm", k]
            e_t = work.tile([P, 4, PACK, P], F32, name="e_t", tag="e_t", bufs=3)
            ssum = small.tile([P, 4], F32, name="ssum", tag="ssum")
            for blk in range(2):
                v = st["t_u", k, blk][:].bitcast(BF16).rearrange("w j (p e) -> w e j p", e=2)
                for e in range(2):
                    i = blk * 2 + e
                    nc.scalar.activation(
                        out=e_t[:, i, :, :], in_=v[:, e, :, :], func=ACT.Exp,
                        bias=negm[:, i : i + 1], scale=1.0, accum_out=ssum[:, i : i + 1],
                    )
            st["e_t", k] = e_t
            st["ssum", k] = ssum

        def centre(k, engines):
            b, t0 = where(k)
            if st.get(("ym", k)) is None:
                st["ym", k] = work.tile([P, PACK, TC], F32, name="ym", tag="ym")
            ym = st["ym", k]
            for j, engine in enumerate(engines):
                if engine == "S":
                    nc.scalar.activation(
                        out=ym[:, j, :], in_=y[b][:, j, t0 : t0 + TC], func=ACT.Identity,
                        bias=negmean[b][:, j : j + 1], scale=1.0,
                    )
                elif engine == "V":
                    nc.vector.tensor_scalar(
                        out=ym[:, j, :], in0=y[b][:, j, t0 : t0 + TC],
                        scalar1=negmean[b][:, j : j + 1], scalar2=None, op0=ALU.add,
                    )
                elif engine == "G":
                    nc.gpsimd.tensor_scalar(
                        out=ym[:, j, :], in0=y[b][:, j, t0 : t0 + TC],
                        scalar1=negmean[b][:, j : j + 1], scalar2=1.0, op0=ALU.add, op1=ALU.mult,
                    )

        def recip(k):
            rinv = small.tile([P, 4], F32, name="rinv", tag="rinv")
            nc.vector.reciprocal(out=rinv[:], in_=st["ssum", k][:])
            st["rinv", k] = rinv

        def normalise(k, quarters=(0, 1, 2, 3)):
            rinv = st["rinv", k]
            e_t = st["e_t", k]
            for i in quarters:
                nc.gpsimd.tensor_scalar(
                    out=e_t[:, i, :, :], in0=e_t[:, i, :, :],
                    scalar1=rinv[:, i : i + 1], scalar2=0.0, op0=ALU.mult, op1=ALU.add,
                )

        def back(k, i):
            e_t = st["e_t", k]
            s_b = psum.tile([P, PACK, P], F32, name="s_b", tag="s_b")
            for j in range(PACK):
                nc.tensor.transpose(s_b[:, j, :], e_t[:, i, j, :], ident[:])
            st["s_b", k, i] = s_b

        def product(k, i):
            if i == 0:
                st["a_g", k] = work.tile([P, TC, PACK], BF16, name="a_g", tag="a_g", bufs=1, align_bytes=64)
            a_g = st["a_g", k]
            ymv = st["ym", k][:].rearrange("p j (b w e) -> p b e w j", b=2, e=2)
            blk, e = divmod(i, 2)
            n0 = e * 256 + blk * P
            nc.vector.tensor_tensor(
                out=a_g[:, n0 : n0 + P, :].rearrange("p (c i) j -> p c j i", i=4),
                in0=ymv[:, blk, e, :, :].rearrange("p (c i) j -> p c j i", i=4),
                in1=st["s_b", k, i][:].rearrange("p j (c i) -> p c j i", i=4), op=ALU.mult,
            )

        def quantise(k):
            codes = work.tile([P, TC], U32, name="codes", tag="codes", bufs=1, align_bytes=64)
            scales = work.tile([P, TC], U8, name="scales", tag="scales", bufs=1, align_bytes=64)
            nc.vector.quantize_mx(
                out=codes[:].bitcast(FP8X4), scales=scales[:],
                in_=st["a_g", k][:].rearrange("p n j -> p (n j)"),
            )
            st["codes", k] = codes
            st["scales", k] = scales

        def multiply(k, jb):
            acc = psum.tile([P, TC], F32, name="acc", tag="acc", bufs=4)
            nc.tensor.matmul_mx(
                out=acc[:],
                lhsT=w_codes[:, jb * P : (jb + 1) * P].bitcast(FP8X4),
                lhsT_scale=w_scales[:, jb * P : (jb + 1) * P],
                rhs=st["codes", k][:].bitcast(FP8X4), rhs_scale=st["scales", k][:],
                start=True, stop=True,
            )
            st["acc", k, jb] = acc

        def span(k, jb):
            for first in JOINED[jb // 2]:
                if first <= k <= first + 1:
                    return first, 2
            return k, 1

        def part(name, k, jb):
            first, n = span(k, jb)
            if k == first:
                st[name, first, jb] = outp.tile([P, n * TC], F32, name=name, tag=name, bufs=8 if name == "ytr" else 7, align_bytes=64)
            return st[name, first, jb][:, (k - first) * TC : (k - first + 1) * TC]

        def residual(k, jb):
            b, t0 = where(k)
            nc.vector.scalar_tensor_tensor(
                out=part("ytr", k, jb).rearrange("m (w e) -> m w e", e=2),
                in0=z[b][:, jb, t0 : t0 + TC].rearrange("m (w e) -> m w e", e=2),
                scalar=mean[b][:, jb : jb + 1],
                in1=st["acc", k, jb][:].rearrange("m (e w) -> m w e", e=2),
                op0=ALU.subtract, op1=ALU.subtract,
            )

        def representation(k, jb):
            b, t0 = where(k)
            nc.scalar.activation(
                out=part("rep", k, jb).rearrange("m (w e) -> m w e", e=2),
                in_=st["acc", k, jb][:].rearrange("m (e w) -> m w e", e=2),
                func=ACT.Identity, bias=mean[b][:, jb : jb + 1], scale=1.0,
            )

        def store_part(k, jb, block, name):
            first, n = span(k, jb)
            if k == first + n - 1:
                b, t0 = where(first)
                nc.sync.dma_start(out=out_rows(block, b)[:, jb, t0 : t0 + n * TC], in_=st[name, first, jb][:])

        todo = list(range(B * PACK))
        io = {}

        def intensity_first(j):
            io[j] = outp.tile([P, T], F32, name="io", tag="io", bufs=3)
            nc.scalar.activation(out=io[j][:, 0:TC], in_=u_first[:, j, :], func=ACT.Exp)

        def intensity():
            b, j = divmod(todo[0], PACK)
            todo[:1] = []
            if b == 0:
                if j not in io:
                    intensity_first(j)
                nc.scalar.activation(out=io[j][:, TC:T], in_=u_rest[:, j, :], func=ACT.Exp)
            else:
                io[j] = outp.tile([P, T], F32, name="io", tag="io", bufs=3)
                nc.scalar.activation(out=io[j][:], in_=u_second[:, j, :], func=ACT.Exp)
            nc.sync.dma_start(out=out_rows(1, b)[:, j, :], in_=io[j][:])
            if len(later) > 1:
                next_load()

        def fill(ops, on_scalar):
            for op in ops:
                if op == "I":
                    intensity()
                elif on_scalar:
                    mean_scalar(1, op)
                else:
                    mean_vector(1, op)

        def leave(k, q):
            residual(k, q)
            if k >= FINE:
                store_part(k, q, 2, "ytr")

        max_j(0)
        max_j2(0)
        max_t(0)
        u_t(0, 0)
        for j in range(3):
            intensity_first(j)
        max_p(0)
        u_t(0, 1)
        exps(0)
        max_j(1)
        max_j2(1)
        max_t(1)
        u_t(1, 0)
        max_j(2)
        max_j2(2)
        max_t(2)
        max_p(1)
        u_t(1, 1)
        intensity()
        recip(0)
        normalise(0)
        exps(1)
        intensity()
        fold(0, 3)
        for j in range(PACK - 1):
            mean_vector(0, j)
        mean_folded(0, 3)
        max_p(2)
        mean_finish(0)
        max_j(3)
        centre(0, "VVSS")
        max_j2(3)
        recip(1)
        normalise(1)
        centre(1, "--GG")
        back(0, 0)
        back(0, 1)
        u_t(2, 0)
        u_t(2, 1)
        group_w()
        for k in range(NK + 1):
            last = k - 1 >= FINE
            if ok(k + 2) and k + 2 > 0:
                exps(k + 2)
            if ok(k):
                product(k, 0)
                back(k, 2)
                product(k, 1)
                back(k, 3)
            if ok(k + 3):
                max_t(k + 3)
                u_t(k + 3, 0)
            if ok(k - 1):
                representation(k - 1, 3)
                store_part(k - 1, 3, 0, "rep")
                leave(k - 1, 0)
                leave(k - 1, 1)
                if k < NK - 1:
                    leave(k - 1, 2)
                for jb in (0, 1):
                    representation(k - 1, jb)
                    store_part(k - 1, jb, 0, "rep")
            if k in (1, 2):
                fold(1, k - 1)
            if ok(k):
                product(k, 2)
            if ok(k + 1):
                back(k + 1, 0)
            if ok(k):
                product(k, 3)
            if ok(k + 1):
                back(k + 1, 1)
            if ok(k + 3):
                max_p(k + 3)
                u_t(k + 3, 1)
            if ok(k - 1) and k < NK - 1:
                leave(k - 1, 3)
                representation(k - 1, 2)
                store_part(k - 1, 2, 0, "rep")
            if k - 1 == Z1_AFTER:
                next_load()
            fill(V_FILL.get(k, ()), False)
            fill(S_FILL.get(k, ()), True)
            if k == 0:
                quantise_w()
            if ok(k):
                quantise(k)
            if k == 0:
                centre(1, "VV--")
            if ok(k + 4):
                max_j(k + 4)
            if k == 2:
                mean_finish(1)
            if ok(k + 2) and k + 2 > 0:
                centre(k + 2, "VV--")
            if ok(k + 4):
                max_j2(k + 4)
            if ok(k - 1) and k >= NK - 1:
                leave(k - 1, 2)
                representation(k - 1, 2)
                store_part(k - 1, 2, 0, "rep")
                leave(k - 1, 3)
            if ok(k):
                for jb in range(4):
                    multiply(k, jb)
            if ok(k + 2) and k + 2 > 0:
                recip(k + 2)
                normalise(k + 2, (0, 1))
                centre(k + 2, "--GG")
                normalise(k + 2, (2, 3))
